import numpy as np
import ml_dtypes


def mxq(x, axis, fmt="e4m3"):
    dtype, down = {"e4m3": (ml_dtypes.float8_e4m3fn, 7), "e5m2": (ml_dtypes.float8_e5m2, 14)}[fmt]
    v = np.moveaxis(np.asarray(x, np.float32).astype(ml_dtypes.bfloat16).astype(np.float64), axis, -1)
    blocks = v.reshape(v.shape[:-1] + (-1, 32))
    amax = np.abs(blocks).max(-1, keepdims=True)
    byte = np.maximum(np.where(amax > 0, np.frexp(amax)[1] - 1 + 127, 0) - down, 1)
    scale = np.exp2(byte - 127.0)
    codes = (blocks / scale).astype(np.float32).astype(dtype).astype(np.float64)
    return np.moveaxis((codes * scale).reshape(v.shape), -1, axis)


WIDE = False


def mx_kscale(k):
    if not WIDE:
        return np.ones(k)
    levels = np.array([10, -10, 5, -5, 0])
    a = np.random.permutation(np.resize(levels, k // 512 * 4)).reshape(k // 512, 4)
    idx = np.arange(k)
    return np.exp2(a[idx // 512, idx % 128 // 32])


BF16 = ml_dtypes.bfloat16


def bf(x):
    return np.asarray(x, np.float32).astype(BF16)


def f64(x):
    return np.asarray(x).astype(np.float64)


NM, B, IN, H1, H2, OUT = 8, 128, 512, 512, 512, 128
LS_LO, LS_HI = -20.0, 4.0
MIN_LS, MAX_LS = -20.0, 2.0


def fnoise(ei, ej):
    return np.sign(ei) * np.sign(ej) * np.sqrt(np.abs(ei)) * np.sqrt(np.abs(ej))


def plin(xq, w, b):
    y = xq.transpose(1, 0, 2) @ mxq(f64(w), 2, 'e4m3').transpose(0, 2, 1)
    return y.transpose(1, 0, 2) + f64(b)[None]


def setup_inputs():
    k = mx_kscale(H1)
    t = mx_kscale(H2)
    return {'x1': bf(np.maximum(np.random.standard_normal((B, NM, H1)) * 3.5, 0.0) * k),
            'ei2': bf(np.random.standard_normal((B, NM, 1))),
            'ej2': bf(np.random.standard_normal((1, NM, H2)) * t * t),
            'w21': bf(np.random.standard_normal((NM, H2, H1)) * 0.4 / np.sqrt(H1) / k * t[:, None]),
            'b21': bf(np.random.standard_normal((NM, H2)) * 0.3 * t),
            'w22': bf(np.random.standard_normal((NM, H2, H1)) * 0.48 / np.sqrt(H1) / k),
            'b22': bf(np.random.standard_normal((NM, H2)) * 0.3),
            'w31': bf(np.random.standard_normal((NM, OUT, H2)) * 0.4 / np.sqrt(H2) / t),
            'b31': bf(np.random.standard_normal((NM, OUT)) * 0.3),
            'w32': bf(np.random.standard_normal((NM, OUT, H2)) * 2.4 / np.sqrt(H2) / t),
            'b32': bf(np.random.standard_normal((NM, OUT)) * 2.0 - 9.0)}


def reference(x1, ei2, ej2, w21, b21, w22, b22, w31, b31, w32, b32):
    x1q = mxq(f64(x1), 2, 'e4m3')
    mu = plin(x1q, w21, b21)
    log_sigma = np.clip(plin(x1q, w22, b22), LS_LO, LS_HI)
    x2 = np.maximum(mu + fnoise(f64(ei2), f64(ej2)) * np.exp(log_sigma), 0.0)
    x2q = mxq(x2, 2, 'e4m3')
    m = plin(x2q, w31, b31)
    log_stdev = np.clip(plin(x2q, w32, b32), MIN_LS, MAX_LS)
    return m, log_stdev

@@ -1,0 +1,532 @@
+from contextlib import ExitStack
+
+import concourse.mybir as mybir
+from concourse.masks import make_identity
+
+F32 = mybir.dt.float32
+BF16 = mybir.dt.bfloat16
+U32 = mybir.dt.uint32
+U8 = mybir.dt.uint8
+FP8X4 = mybir.dt.float8_e4m3fn_x4
+ALU = mybir.AluOpType
+ACT = mybir.ActivationFunctionType
+
+P = 128
+NM = 8
+K = 512
+OUT = 128
+FLOPS = 2 * 128 * NM * (2 * 512 * 512 + 2 * 512 * 128)
+
+N_TP = 4
+N_G2 = 6
+N_C2 = 6
+N_G3 = 4
+HOP = 80.0
+SWITCH = 90.0
+
+
+def plan(units, names, landed):
+    done = dict(landed)
+    where = {}
+    free = {"pe": 0.0, "act": 0.0, "dve": 0.0, "pool": 0.0}
+    bank_free = [0.0] * N_TP
+    bank_open = [True] * N_TP
+    bank_of = {}
+    todo = list(names)
+    seq = []
+    kind = [""]
+    while todo:
+        best = None
+        for name in todo:
+            u = units[name]
+            ready = all(d in done for d in u["deps"])
+            if not ready:
+                continue
+            for eng in u["engines"]:
+                t = 0.0
+                for d in u["deps"]:
+                    lag = 0.0 if where.get(d, "") == eng else HOP
+                    if d in units:
+                        lag += units[d]["after"]
+                    t = max(t, done[d] + lag)
+                bank = -1
+                if u["bank"] == "take":
+                    cands = [s for s in range(N_TP) if bank_open[s]]
+                    if not cands:
+                        continue
+                    bank = min(cands, key=lambda s: bank_free[s])
+                    t = max(t, bank_free[bank] + HOP)
+                start = max(t, free[eng])
+                key = (start, u["prio"])
+                if best is None or key < best[0]:
+                    best = (key, name, eng, bank)
+        assert best is not None, "the plan is stuck"
+        key, name, eng, bank = best
+        u = units[name]
+        cost = u["cost"]
+        if eng == "pe":
+            if kind[0] != "" and kind[0] != u["kind"]:
+                cost += SWITCH
+            kind[0] = u["kind"]
+        end = key[0] + cost
+        done[name] = end
+        where[name] = eng
+        free[eng] = end
+        if bank >= 0:
+            bank_open[bank] = False
+            bank_of[name] = bank
+        if u["bank"] != "" and u["bank"] != "take":
+            b = bank_of[u["bank"]]
+            bank_open[b] = True
+            bank_free[b] = end
+        todo = [n for n in todo if n != name]
+        seq.append((name, eng, bank))
+    return seq
+
+
+def tile_skill_net_pb_kernel(
+    tc, x1, ei2, ej2, w21, b21, w22, b22, w31, b31, w32, b32, out_0, out_1
+):
+    nc = tc.nc
+    with ExitStack() as ctx:
+        ctx.enter_context(tc.manual_schedule())
+        const = ctx.enter_context(tc.tile_pool(name="const", bufs=1))
+        raw = ctx.enter_context(tc.tile_pool(name="raw", bufs=1))
+        work = ctx.enter_context(tc.tile_pool(name="work", bufs=1))
+        psum = ctx.enter_context(tc.psum_pool(name="psum", bufs=1))
+
+        clip_in = const.tile([P, 2], F32, name="clip_in")
+        nc.vector.memset(clip_in[:, 0:1], -20.0)
+        nc.vector.memset(clip_in[:, 1:2], 4.0)
+        rows = const.tile([P, K], BF16, name="rows")
+        ei_sb = const.tile([P, NM], BF16, name="ei_sb")
+        nc.scalar.dma_start(out=ei_sb[:], in_=ei2.rearrange("b j o -> b (j o)"))
+        nc.scalar.dma_start(out=rows[0:8, :], in_=ej2.rearrange("o j h -> (o j) h"))
+        nc.scalar.dma_start(out=rows[8:16, :], in_=b21)
+        nc.scalar.dma_start(out=rows[16:24, :], in_=b22)
+        nc.scalar.dma_start(out=rows[24:32, :], in_=b22)
+        nc.vector.memset(rows[32:64, :], 0.0)
+        nc.vector.memset(rows[64:128, :], 0.0)
+        half = const.tile([P, 40], F32, name="half")
+        nc.vector.memset(half[:], 0.5)
+        clip_e = const.tile([P, 2], F32, name="clip_e")
+        nc.scalar.activation(out=clip_e[:], in_=clip_in[:], func=ACT.Exp)
+        ident = const.tile([P, P], F32, name="ident")
+        make_identity(nc, ident[:])
+
+        x1_sb = [raw.tile([P, 2, K], BF16, name="x1_sb%d" % q) for q in range(4)]
+        w2_sb = [[raw.tile([P, 4, K], BF16, name="w2_sb%d_%d" % (m, j)) for j in range(NM)] for m in range(2)]
+        w3_sb = [[raw.tile([P, 2, K], BF16, name="w3_sb%d_%d" % (m, q)) for q in range(4)] for m in range(2)]
+        bias3 = const.tile([P, NM, 2, OUT], BF16, name="bias3")
+        w2_dram = (w21, w22)
+        w3_dram = (w31, w32)
+        landed = {}
+        clock = [2000.0]
+
+        def lands(name, kib):
+            clock[0] += kib / 0.56
+            landed[name] = clock[0]
+
+        def load_x1(q):
+            nc.sync.dma_start(out=x1_sb[q][:], in_=x1[:, 2 * q : 2 * q + 2, :])
+            lands("x1_%d" % q, 256)
+
+        def load_w2(j):
+            for m in (1, 0):
+                nc.sync.dma_start(out=w2_sb[m][j][:], in_=w2_dram[m][j].rearrange("(p c) k -> p c k", c=4))
+                lands("w2_%d_%d" % (m, j), 512)
+
+        def load_w3(q):
+            for m in range(2):
+                nc.sync.dma_start(
+                    out=w3_sb[m][q][:], in_=w3_dram[m][2 * q : 2 * q + 2].rearrange("j o h -> o j h")
+                )
+            lands("w3_%d" % q, 512)
+
+        def load_bias3():
+            nc.sync.dma_start(out=bias3[:, :, 0, :], in_=b31.partition_broadcast(P))
+            nc.sync.dma_start(out=bias3[:, :, 1, :], in_=b32.partition_broadcast(P))
+            lands("bias3", 512)
+
+        landed["small"] = 3000.0
+        load_x1(0)
+        load_w2(0)
+        load_w2(1)
+        load_x1(1)
+        load_w3(0)
+        load_w2(2)
+        load_bias3()
+        load_w2(3)
+        load_x1(2)
+        load_w3(1)
+        load_w2(4)
+        load_w2(5)
+        load_x1(3)
+        load_w3(2)
+        load_w2(6)
+        load_w2(7)
+        load_w3(3)
+
+        units = {}
+        names = []
+        banks = {}
+
+        def unit(name, engines, cost, prio, deps, emit, bank="", kind="", after=0.0):
+            units[name] = {
+                "engines": engines,
+                "cost": cost,
+                "prio": prio,
+                "deps": deps,
+                "emit": emit,
+                "bank": bank,
+                "kind": kind,
+                "after": after,
+            }
+            names.append(name)
+
+        def copy_out(eng, out, in_):
+            if eng == "act":
+                nc.scalar.copy(out=out, in_=in_)
+            else:
+                nc.vector.tensor_copy(out=out, in_=in_)
+
+        def new_bank(name, bank):
+            banks[name] = psum.tile([P, 4, P], F32, name="tp", tag="tp%d" % bank)
+            return banks[name]
+
+        vec_bf = const.tile([P, 96], BF16, name="vec_bf")
+        noise_in = const.tile([P, 40], F32, name="noise_in")
+        bias12 = const.tile([P, 2, NM, 4], F32, name="bias12")
+        mag = const.tile([P, 40], F32, name="mag")
+        neg = const.tile([P, 40], F32, name="neg")
+        sgn = const.tile([P, 40], F32, name="sgn")
+        root = const.tile([P, 40], F32, name="root")
+        fac = const.tile([P, 40], F32, name="fac")
+        fi_all = const.tile([P, NM, P], F32, name="fi_all")
+
+        def emit_tr(eng, bank):
+            rt = new_bank("TR", bank)
+            rows_w = rows[:].bitcast(F32).rearrange("r (q u) -> r q u", u=2)
+            for u in range(2):
+                nc.tensor.transpose(rt[:, u, :], rows_w[:, :, u], ident[:])
+
+        def emit_evr(eng, bank):
+            nc.vector.tensor_copy(
+                out=vec_bf[:].bitcast(F32).rearrange("p (r u) -> p r u", u=2),
+                in_=banks["TR"][:, 0:2, 0:24].rearrange("p u r -> p r u"),
+            )
+
+        def emit_chain(eng, bank):
+            nc.vector.tensor_copy(out=noise_in[:, 0:8], in_=ei_sb[:])
+            nc.vector.tensor_copy(out=noise_in[:, 8:40], in_=vec_bf[:, 0:32])
+            nc.vector.scalar_tensor_tensor(
+                out=mag[:], in0=noise_in[:], scalar=-1.0, in1=noise_in[:], op0=ALU.mult, op1=ALU.max
+            )
+            nc.vector.tensor_scalar_max(out=mag[:], in0=mag[:], scalar1=2.0 ** -116)
+
+        def emit_sign(eng, bank):
+            nc.vector.tensor_single_scalar(out=neg[:], in_=noise_in[:], scalar=0.0, op=ALU.is_lt)
+            nc.vector.scalar_tensor_tensor(
+                out=sgn[:], in0=noise_in[:], scalar=0.0, in1=neg[:], op0=ALU.is_gt, op1=ALU.subtract
+            )
+            nc.vector.tensor_copy(out=bias12[:].rearrange("p m j c -> p (m j c)"), in_=vec_bf[:, 32:96])
+
+        unit("TR", ("pe",), 210, -100, ["small"], emit_tr, bank="take", kind="t")
+        unit("EVR", ("dve",), 100, -100, ["TR"], emit_evr, bank="TR")
+        unit("chain", ("dve",), 260, -99, ["EVR"], emit_chain)
+        unit("sign", ("dve",), 200, -98, ["chain"], emit_sign)
+        pieces = ((0, 8), (8, 12), (12, 16), (16, 24), (24, 40))
+        for i, (lo, hi) in enumerate(pieces):
+
+            def emit_pow(eng, bank, lo=lo, hi=hi):
+                nc.gpsimd.tensor_tensor(out=root[:, lo:hi], in0=mag[:, lo:hi], in1=half[:, lo:hi], op=ALU.pow)
+
+            def emit_fac(eng, bank, lo=lo, hi=hi):
+                nc.vector.tensor_mul(out=fac[:, lo:hi], in0=root[:, lo:hi], in1=sgn[:, lo:hi])
+
+            unit("pow%d" % i, ("pool",), 150 + 200 * (hi - lo), -97 + i, ["chain"], emit_pow)
+            unit("fac%d" % i, ("dve",), 70, (-97.0, -36.5, 63.5, 163.5, 363.5)[i], ["pow%d" % i, "sign"], emit_fac)
+
+        for h in range(2):
+
+            def emit_tfi(eng, bank, h=h):
+                ft = new_bank("TFI%d" % h, bank)
+                for jj in range(4):
+                    j = 4 * h + jj
+                    nc.tensor.transpose(ft[:, jj, :], fac[:, j : j + 1].to_broadcast([P, P]), ident[:])
+
+            def emit_evfi(eng, bank, h=h):
+                copy_out(eng, fi_all[:, 4 * h : 4 * h + 4, :], banks["TFI%d" % h][:])
+
+            unit("TFI%d" % h, ("pe",), 260, -40 + 245 * h, ["fac0"], emit_tfi, bank="take", kind="t")
+            unit("EVFI%d" % h, ("act", "dve"), 445, -40 + 245 * h, ["TFI%d" % h], emit_evfi, bank="TFI%d" % h)
+
+        x1_g = work.tile([P, NM * K], BF16, name="x1_g", align_bytes=64)
+        x1_gw = x1_g[:].bitcast(F32).rearrange("p (j b u) -> p j b u", j=NM, u=2)
+        x1_c = work.tile([P, NM * P], U32, name="x1_c", align_bytes=64)
+        x1_s = work.tile([P, NM * P], U8, name="x1_s", align_bytes=64)
+        for q in range(4):
+
+            def emit_tx(eng, bank, q=q):
+                xt = new_bank("TX%d" % q, bank)
+                for jj in range(2):
+                    words = x1_sb[q][:, jj, :].bitcast(F32)
+                    for u in range(2):
+                        nc.tensor.transpose(xt[:, 2 * jj + u, :], words[:, P * u : P * u + P], ident[:])
+
+            def emit_evx(eng, bank, q=q):
+                copy_out(
+                    eng,
+                    x1_gw[:, 2 * q : 2 * q + 2],
+                    banks["TX%d" % q][:].rearrange("p (j u) b -> p j b u", u=2),
+                )
+
+            def emit_qx(eng, bank, q=q):
+                nc.vector.quantize_mx(
+                    out=x1_c[:, 256 * q : 256 * q + 256].bitcast(FP8X4),
+                    scales=x1_s[:, 256 * q : 256 * q + 256],
+                    in_=x1_g[:, 1024 * q : 1024 * q + 1024],
+                )
+
+            pr = 200 * q - 60
+            unit("TX%d" % q, ("pe",), 260, pr, ["x1_%d" % q], emit_tx, bank="take", kind="t")
+            unit("EVX%d" % q, ("act", "dve"), 445, pr, ["TX%d" % q], emit_evx, bank="TX%d" % q, after=100.0)
+            unit("QX%d" % q, ("dve",), 240, pr, ["EVX%d" % q], emit_qx, after=100.0)
+
+        g2 = {}
+        q2 = {}
+        g3 = {}
+        q3 = {}
+        acc = {}
+        tmp = {}
+        x2q = {}
+        ps2 = {}
+        res = {}
+        for j in range(NM):
+            base = 100 * j
+            for m, off in ((1, 0), (0, 5)):
+                idx = 2 * j + (1 - m)
+                for hf in range(2):
+
+                    def emit_t2(eng, bank, j=j, m=m, hf=hf):
+                        xt = new_bank("T%d_%d_%d" % (m, j, hf), bank)
+                        for cc in range(2):
+                            words = w2_sb[m][j][:, 2 * hf + cc, :].bitcast(F32)
+                            for u in range(2):
+                                nc.tensor.transpose(xt[:, 2 * cc + u, :], words[:, P * u : P * u + P], ident[:])
+
+                    def emit_ev2(eng, bank, j=j, m=m, hf=hf, idx=idx):
+                        if (j, m) not in g2:
+                            g2[(j, m)] = work.tile(
+                                [P, 4 * K], BF16, name="w2_g", tag="w2_g%d" % (idx % N_G2), align_bytes=64
+                            )
+                        gw = g2[(j, m)][:].bitcast(F32).rearrange("p (c w u) -> p c w u", c=4, u=2)
+                        copy_out(
+                            eng,
+                            gw[:, 2 * hf : 2 * hf + 2],
+                            banks["T%d_%d_%d" % (m, j, hf)][:].rearrange("p (c u) w -> p c w u", u=2),
+                        )
+
+                    tn = "T%d_%d_%d" % (m, j, hf)
+                    deps = [tn]
+                    if idx >= N_G2:
+                        deps.append("Q%d_%d" % (1 - (idx - N_G2) % 2, (idx - N_G2) // 2))
+                    unit(tn, ("pe",), 260, base - 50 + off + hf, ["w2_%d_%d" % (m, j)], emit_t2, bank="take", kind="t")
+                    unit("EV%d_%d_%d" % (m, j, hf), ("act", "dve"), 445, base - 50 + off + hf, deps, emit_ev2, bank=tn, after=100.0)
+
+                def emit_q2(eng, bank, j=j, m=m, idx=idx):
+                    codes = work.tile([P, K], U32, name="w2_c", tag="w2_c%d" % (idx % N_C2), align_bytes=64)
+                    scales = work.tile([P, K], U8, name="w2_s", tag="w2_s%d" % (idx % N_C2), align_bytes=64)
+                    nc.vector.quantize_mx(out=codes[:].bitcast(FP8X4), scales=scales[:], in_=g2[(j, m)][:])
+                    q2[(j, m)] = (codes, scales)
+
+                deps = ["EV%d_%d_0" % (m, j), "EV%d_%d_1" % (m, j)]
+                if idx >= N_C2:
+                    deps.append("S1_%d_%d" % (1 - (idx - N_C2) % 2, (idx - N_C2) // 2))
+                unit("Q%d_%d" % (m, j), ("dve",), 477, base - 50 + off + 2, deps, emit_q2, after=100.0)
+
+                def emit_s1(eng, bank, j=j, m=m):
+                    codes, scales = q2[(j, m)]
+                    if m == 1:
+                        ps = psum.tile([P, 4, P], F32, name="ps_ls", tag="ls")
+                    else:
+                        ps = psum.tile([P, 4, P], F32, name="ps_mu", tag="mu%d" % (j % 2))
+                    for c in range(4):
+                        nc.tensor.matmul_mx(
+                            out=ps[:, c, :],
+                            lhsT=codes[:, P * c : P * c + P].bitcast(FP8X4),
+                            lhsT_scale=scales[:, P * c : P * c + P],
+                            rhs=x1_c[:, P * j : P * j + P].bitcast(FP8X4),
+                            rhs_scale=x1_s[:, P * j : P * j + P],
+                            start=True,
+                            stop=True,
+                        )
+                    acc[(j, m)] = ps
+
+                deps = ["Q%d_%d" % (m, j), "QX%d" % (j // 2)]
+                if m == 1 and j >= 1:
+                    deps.append("a_%d" % (j - 1))
+                if m == 0 and j >= 2:
+                    deps.append("d_%d" % (j - 2))
+                unit("S1_%d_%d" % (m, j), ("pe",), 250, base - 40 + (1 - m), deps, emit_s1, kind="m")
+
+            def emit_t3(eng, bank, j=j):
+                xt = new_bank("TW3_%d" % j, bank)
+                for m in range(2):
+                    words = w3_sb[m][j // 2][:, j % 2, :].bitcast(F32).rearrange("o (q u) -> o q u", u=2)
+                    for u in range(2):
+                        nc.tensor.transpose(xt[:, 2 * m + u, :], words[:, :, u], ident[:])
+
+            def emit_ev3(eng, bank, j=j):
+                g3[j] = work.tile([P, 2 * K], BF16, name="w3_g", tag="w3_g%d" % (j % N_G3), align_bytes=64)
+                copy_out(
+                    eng,
+                    g3[j][:].bitcast(F32).rearrange("p (m o u) -> p m o u", m=2, u=2),
+                    banks["TW3_%d" % j][:].rearrange("p (m u) o -> p m o u", u=2),
+                )
+
+            def emit_q3(eng, bank, j=j):
+                codes = work.tile([P, 2 * OUT], U32, name="w3_c%d" % j, align_bytes=64)
+                scales = work.tile([P, 2 * OUT], U8, name="w3_s%d" % j, align_bytes=64)
+                nc.vector.quantize_mx(out=codes[:].bitcast(FP8X4), scales=scales[:], in_=g3[j][:])
+                q3[j] = (codes, scales)
+
+            deps = ["TW3_%d" % j]
+            if j >= N_G3:
+                deps.append("QW3_%d" % (j - N_G3))
+            unit("TW3_%d" % j, ("pe",), 416, base - 20, ["w3_%d" % (j // 2)], emit_t3, bank="take", kind="t")
+            unit("EVW3_%d" % j, ("act", "dve"), 445, base - 20, deps, emit_ev3, bank="TW3_%d" % j, after=100.0)
+            unit("QW3_%d" % j, ("dve",), 240, base - 20, ["EVW3_%d" % j], emit_q3, after=100.0)
+
+            def emit_a(eng, bank, j=j):
+                e = work.tile([P, 4, P], F32, name="e", tag="e%d" % (j % 2))
+                for c in range(4):
+                    nc.scalar.activation(
+                        out=e[:, c, :],
+                        in_=acc[(j, 1)][:, c, :],
+                        func=ACT.Exp,
+                        bias=bias12[:, 1, j, c : c + 1],
+                        scale=1.0,
+                    )
+                tmp[("e", j)] = e
+
+            def emit_b(eng, bank, j=j):
+                t2 = work.tile([P, 4, P], F32, name="t2", tag="t2_%d" % (j % 2))
+                nc.vector.tensor_scalar(
+                    out=t2[:],
+                    in0=tmp[("e", j)][:],
+                    scalar1=clip_e[:, 0:1],
+                    scalar2=clip_e[:, 1:2],
+                    op0=ALU.max,
+                    op1=ALU.min,
+                )
+                tmp[("t2", j)] = t2
+
+            def emit_c(eng, bank, j=j):
+                t4 = work.tile([P, 4, P], F32, name="t4", tag="t4_%d" % (j % 2))
+                for c in range(4):
+                    nc.vector.scalar_tensor_tensor(
+                        out=t4[:, c, :],
+                        in0=tmp[("t2", j)][:, c, :],
+                        scalar=fac[:, 8 + 4 * j + c : 9 + 4 * j + c],
+                        in1=fi_all[:, j, :],
+                        op0=ALU.mult,
+                        op1=ALU.mult,
+                    )
+                tmp[("t4", j)] = t4
+
+            def emit_d(eng, bank, j=j):
+                s = work.tile([P, 4, P], F32, name="s", tag="s%d" % (j % 2))
+                for c in range(4):
+                    nc.vector.scalar_tensor_tensor(
+                        out=s[:, c, :],
+                        in0=acc[(j, 0)][:, c, :],
+                        scalar=bias12[:, 0, j, c : c + 1],
+                        in1=tmp[("t4", j)][:, c, :],
+                        op0=ALU.add,
+                        op1=ALU.add,
+                    )
+                tmp[("s", j)] = s
+
+            def emit_e(eng, bank, j=j):
+                x2_g = work.tile([P, K], BF16, name="x2_g", tag="x2_g%d" % (j % 2), align_bytes=64)
+                if eng == "act":
+                    nc.scalar.activation(
+                        out=x2_g[:].rearrange("p (b c) -> p b c", c=4),
+                        in_=tmp[("s", j)][:].rearrange("p c b -> p b c"),
+                        func=ACT.Relu,
+                    )
+                else:
+                    nc.vector.tensor_scalar_max(
+                        out=x2_g[:].rearrange("p (b c) -> p b c", c=4),
+                        in0=tmp[("s", j)][:].rearrange("p c b -> p b c"),
+                        scalar1=0.0,
+                    )
+                tmp[("x2", j)] = x2_g
+
+            def emit_qx2(eng, bank, j=j):
+                codes = work.tile([P, P], U32, name="x2_c%d" % j, align_bytes=64)
+                scales = work.tile([P, P], U8, name="x2_s%d" % j, align_bytes=64)
+                nc.vector.quantize_mx(out=codes[:].bitcast(FP8X4), scales=scales[:], in_=tmp[("x2", j)][:])
+                x2q[j] = (codes, scales)
+
+            def emit_s2(eng, bank, j=j):
+                if j % 2 == 0:
+                    ps2[j // 2] = psum.tile([P, 2, 2 * OUT], F32, name="ps2", tag="ps2")
+                codes, scales = x2q[j]
+                wc, ws = q3[j]
+                nc.tensor.matmul_mx(
+                    out=ps2[j // 2][:, j % 2, :],
+                    lhsT=codes[:].bitcast(FP8X4),
+                    lhsT_scale=scales[:],
+                    rhs=wc[:].bitcast(FP8X4),
+                    rhs_scale=ws[:],
+                    start=True,
+                    stop=True,
+                )
+
+            def emit_out(eng, bank, j=j):
+                q = j // 2
+                if j % 2 == 0:
+                    res[q] = work.tile([P, 2, 2, OUT], F32, name="res%d" % q)
+                r = res[q]
+                nc.vector.tensor_tensor(
+                    out=r[:, j % 2].rearrange("p m o -> p (m o)"),
+                    in0=ps2[q][:, j % 2, :],
+                    in1=bias3[:, j].rearrange("p m o -> p (m o)"),
+                    op=ALU.add,
+                )
+                nc.vector.tensor_scalar(
+                    out=r[:, j % 2, 1, :], in0=r[:, j % 2, 1, :], scalar1=-20.0, scalar2=2.0, op0=ALU.max, op1=ALU.min
+                )
+                if q == 3:
+                    nc.sync.dma_start(out=out_0[:, j, :], in_=r[:, j % 2, 0, :])
+                    nc.sync.dma_start(out=out_1[:, j, :], in_=r[:, j % 2, 1, :])
+                elif j % 2 == 1:
+                    nc.sync.dma_start(out=out_0[:, 2 * q : 2 * q + 2, :], in_=r[:, :, 0, :])
+                    nc.sync.dma_start(out=out_1[:, 2 * q : 2 * q + 2, :], in_=r[:, :, 1, :])
+
+            def older(name, back):
+                return [name % (j - back)] if j >= back else []
+
+            unit("a_%d" % j, ("act",), 600, base - 38, ["S1_1_%d" % j, "sign"] + older("b_%d", 2), emit_a)
+            unit("b_%d" % j, ("dve",), 226, base - 37, ["a_%d" % j] + older("c_%d", 2), emit_b)
+            unit(
+                "c_%d" % j,
+                ("dve",),
+                480,
+                base - 36,
+                ["b_%d" % j, "EVFI%d" % (j // 4), "fac%d" % (1 + min(j, 2) + (j // 4))] + older("d_%d", 2),
+                emit_c,
+            )
+            unit("d_%d" % j, ("dve",), 480, base - 35, ["c_%d" % j, "S1_0_%d" % j] + older("e_%d", 2), emit_d)
+            unit("e_%d" % j, ("act",), 550, base - 34, ["d_%d" % j] + older("qx2_%d", 2), emit_e)
+            unit("qx2_%d" % j, ("dve",), 140, base - 33, ["e_%d" % j], emit_qx2, after=150.0)
+            deps = ["qx2_%d" % j, "QW3_%d" % j]
+            if j % 2 == 0 and j >= 2:
+                deps += ["OUT_%d" % (j - 1), "OUT_%d" % (j - 2)]
+            unit("S2_%d" % j, ("pe",), 111, base - 32, deps, emit_s2, kind="m")
+            unit("OUT_%d" % j, ("dve",), 300, base - 31, ["S2_%d" % j, "bias3"], emit_out)
+
+        for name, eng, bank in plan(units, names, landed):
+            units[name]["emit"](eng, bank)

@@ -113,11 +113,15 @@ def tile_skill_net_pb_kernel(
         nc.scalar.activation(out=clip_e[:], in_=clip_in[:], func=ACT.Exp)
         ident = const.tile([P, P], F32, name="ident")
         make_identity(nc, ident[:])
+        ident_bf = const.tile([P, P], BF16, name="ident_bf")
+        nc.vector.tensor_copy(out=ident_bf[:], in_=ident[:])
 
         x1_sb = [raw.tile([P, 2, K], BF16, name="x1_sb%d" % q) for q in range(4)]
         w2_sb = [[raw.tile([P, 4, K], BF16, name="w2_sb%d_%d" % (m, j)) for j in range(NM)] for m in range(2)]
         w3_sb = [[raw.tile([P, 2, K], BF16, name="w3_sb%d_%d" % (m, q)) for q in range(4)] for m in range(2)]
-        bias3 = const.tile([P, NM, 2, OUT], BF16, name="bias3")
+        bias3 = const.tile([P, 2, NM, OUT], BF16, name="bias3")
+        head_rows = const.tile([P, K], BF16, name="head_rows")
+        nc.vector.memset(head_rows[:].bitcast(mybir.dt.int32), 0)
         w2_dram = (w21, w22)
         w3_dram = (w31, w32)
         landed = {}
@@ -143,19 +147,19 @@ def tile_skill_net_pb_kernel(
                 )
             lands("w3_%d" % q, 512)
 
-        def load_bias3():
-            nc.sync.dma_start(out=bias3[:, :, 0, :], in_=b31.partition_broadcast(P))
-            nc.sync.dma_start(out=bias3[:, :, 1, :], in_=b32.partition_broadcast(P))
-            lands("bias3", 512)
+        def load_head_rows():
+            nc.scalar.dma_start(out=head_rows[0:2, :], in_=b31.rearrange("(r j) o -> r (j o)", r=2))
+            nc.scalar.dma_start(out=head_rows[2:4, :], in_=b32.rearrange("(r j) o -> r (j o)", r=2))
+            landed["head_rows"] = 4500.0
 
         landed["small"] = 3000.0
         load_x1(0)
         load_w2(0)
+        load_head_rows()
         load_w2(1)
         load_x1(1)
         load_w3(0)
         load_w2(2)
-        load_bias3()
         load_w2(3)
         load_x1(2)
         load_w3(1)
@@ -260,6 +264,25 @@ def tile_skill_net_pb_kernel(
 
             unit("TFI%d" % h, ("pe",), 260, -40 + 245 * h, ["fac0"], emit_tfi, bank="take", kind="t")
             unit("EVFI%d" % h, ("act", "dve"), 445, -40 + 245 * h, ["TFI%d" % h], emit_evfi, bank="TFI%d" % h)
+
+        for r in range(4):
+
+            def emit_tb(eng, bank, r=r):
+                bt = new_bank("TB%d" % r, bank)
+                nc.tensor.matmul(
+                    out=bt[:].rearrange("p j o -> p (j o)"),
+                    lhsT=ident_bf[:, r : r + 1].to_broadcast([P, P]),
+                    rhs=head_rows[:],
+                    start=True,
+                    stop=True,
+                )
+
+            def emit_evb(eng, bank, r=r):
+                copy_out(eng, bias3[:, r // 2, 4 * (r % 2) : 4 * (r % 2) + 4, :], banks["TB%d" % r][:])
+
+            pr = -30 + 400 * (r % 2)
+            unit("TB%d" % r, ("pe",), 230, pr, ["head_rows"], emit_tb, bank="take", kind="t")
+            unit("EVB%d" % r, ("act", "dve"), 445, pr, ["TB%d" % r], emit_evb, bank="TB%d" % r)
 
         x1_g = work.tile([P, NM * K], BF16, name="x1_g", align_bytes=64)
         x1_gw = x1_g[:].bitcast(F32).rearrange("p (j b u) -> p j b u", j=NM, u=2)
@@ -491,9 +514,9 @@ def tile_skill_net_pb_kernel(
                     res[q] = work.tile([P, 2, 2, OUT], F32, name="res%d" % q)
                 r = res[q]
                 nc.vector.tensor_tensor(
-                    out=r[:, j % 2].rearrange("p m o -> p (m o)"),
-                    in0=ps2[q][:, j % 2, :],
-                    in1=bias3[:, j].rearrange("p m o -> p (m o)"),
+                    out=r[:, j % 2],
+                    in0=ps2[q][:, j % 2, :].rearrange("p (m o) -> p m o", m=2),
+                    in1=bias3[:, :, j, :],
                     op=ALU.add,
                 )
                 nc.vector.tensor_scalar(
@@ -526,7 +549,7 @@ def tile_skill_net_pb_kernel(
             if j % 2 == 0 and j >= 2:
                 deps += ["OUT_%d" % (j - 1), "OUT_%d" % (j - 2)]
             unit("S2_%d" % j, ("pe",), 111, base - 32, deps, emit_s2, kind="m")
-            unit("OUT_%d" % j, ("dve",), 300, base - 31, ["S2_%d" % j, "bias3"], emit_out)
+            unit("OUT_%d" % j, ("dve",), 300, base - 31, ["S2_%d" % j, "EVB%d" % (j // 4), "EVB%d" % (2 + j // 4)], emit_out)
 
         for name, eng, bank in plan(units, names, landed):
             units[name]["emit"](eng, bank)

@@ -21,6 +21,7 @@ N_TP = 4
 N_G2 = 6
 N_C2 = 6
 N_G3 = 4
+N_JUNK = 2
 HOP = 80.0
 SWITCH = 90.0
 
@@ -113,15 +114,11 @@ def tile_skill_net_pb_kernel(
         nc.scalar.activation(out=clip_e[:], in_=clip_in[:], func=ACT.Exp)
         ident = const.tile([P, P], F32, name="ident")
         make_identity(nc, ident[:])
-        ident_bf = const.tile([P, P], BF16, name="ident_bf")
-        nc.vector.tensor_copy(out=ident_bf[:], in_=ident[:])
 
         x1_sb = [raw.tile([P, 2, K], BF16, name="x1_sb%d" % q) for q in range(4)]
         w2_sb = [[raw.tile([P, 4, K], BF16, name="w2_sb%d_%d" % (m, j)) for j in range(NM)] for m in range(2)]
         w3_sb = [[raw.tile([P, 2, K], BF16, name="w3_sb%d_%d" % (m, q)) for q in range(4)] for m in range(2)]
-        bias3 = const.tile([P, 2, NM, OUT], BF16, name="bias3")
-        head_rows = const.tile([P, K], BF16, name="head_rows")
-        nc.vector.memset(head_rows[:].bitcast(mybir.dt.int32), 0)
+        bias3 = const.tile([P, NM, 2, OUT], BF16, name="bias3")
         w2_dram = (w21, w22)
         w3_dram = (w31, w32)
         landed = {}
@@ -147,19 +144,19 @@ def tile_skill_net_pb_kernel(
                 )
             lands("w3_%d" % q, 512)
 
-        def load_head_rows():
-            nc.scalar.dma_start(out=head_rows[0:2, :], in_=b31.rearrange("(r j) o -> r (j o)", r=2))
-            nc.scalar.dma_start(out=head_rows[2:4, :], in_=b32.rearrange("(r j) o -> r (j o)", r=2))
-            landed["head_rows"] = 4500.0
+        def load_bias3():
+            nc.sync.dma_start(out=bias3[:, :, 0, :], in_=b31.partition_broadcast(P))
+            nc.sync.dma_start(out=bias3[:, :, 1, :], in_=b32.partition_broadcast(P))
+            lands("bias3", 512)
 
         landed["small"] = 3000.0
         load_x1(0)
         load_w2(0)
-        load_head_rows()
         load_w2(1)
         load_x1(1)
         load_w3(0)
         load_w2(2)
+        load_bias3()
         load_w2(3)
         load_x1(2)
         load_w3(1)
@@ -265,25 +262,6 @@ def tile_skill_net_pb_kernel(
             unit("TFI%d" % h, ("pe",), 260, -40 + 245 * h, ["fac0"], emit_tfi, bank="take", kind="t")
             unit("EVFI%d" % h, ("act", "dve"), 445, -40 + 245 * h, ["TFI%d" % h], emit_evfi, bank="TFI%d" % h)
 
-        for r in range(4):
-
-            def emit_tb(eng, bank, r=r):
-                bt = new_bank("TB%d" % r, bank)
-                nc.tensor.matmul(
-                    out=bt[:].rearrange("p j o -> p (j o)"),
-                    lhsT=ident_bf[:, r : r + 1].to_broadcast([P, P]),
-                    rhs=head_rows[:],
-                    start=True,
-                    stop=True,
-                )
-
-            def emit_evb(eng, bank, r=r):
-                copy_out(eng, bias3[:, r // 2, 4 * (r % 2) : 4 * (r % 2) + 4, :], banks["TB%d" % r][:])
-
-            pr = -30 + 400 * (r % 2)
-            unit("TB%d" % r, ("pe",), 230, pr, ["head_rows"], emit_tb, bank="take", kind="t")
-            unit("EVB%d" % r, ("act", "dve"), 445, pr, ["TB%d" % r], emit_evb, bank="TB%d" % r)
-
         x1_g = work.tile([P, NM * K], BF16, name="x1_g", align_bytes=64)
         x1_gw = x1_g[:].bitcast(F32).rearrange("p (j b u) -> p j b u", j=NM, u=2)
         x1_c = work.tile([P, NM * P], U32, name="x1_c", align_bytes=64)
@@ -374,6 +352,16 @@ def tile_skill_net_pb_kernel(
                         ps = psum.tile([P, 4, P], F32, name="ps_ls", tag="ls")
                     else:
                         ps = psum.tile([P, 4, P], F32, name="ps_mu", tag="mu%d" % (j % 2))
+                    for rep in range(N_JUNK):
+                        nc.tensor.matmul_mx(
+                            out=ps[:].rearrange("p c b -> p (c b)"),
+                            lhsT=codes[:, 0:P].bitcast(FP8X4),
+                            lhsT_scale=scales[:, 0:P],
+                            rhs=codes[:].bitcast(FP8X4),
+                            rhs_scale=scales[:],
+                            start=True,
+                            stop=True,
+                        )
                     for c in range(4):
                         nc.tensor.matmul_mx(
                             out=ps[:, c, :],
@@ -514,9 +502,9 @@ def tile_skill_net_pb_kernel(
                     res[q] = work.tile([P, 2, 2, OUT], F32, name="res%d" % q)
                 r = res[q]
                 nc.vector.tensor_tensor(
-                    out=r[:, j % 2],
-                    in0=ps2[q][:, j % 2, :].rearrange("p (m o) -> p m o", m=2),
-                    in1=bias3[:, :, j, :],
+                    out=r[:, j % 2].rearrange("p m o -> p (m o)"),
+                    in0=ps2[q][:, j % 2, :],
+                    in1=bias3[:, j].rearrange("p m o -> p (m o)"),
                     op=ALU.add,
                 )
                 nc.vector.tensor_scalar(
@@ -549,7 +537,7 @@ def tile_skill_net_pb_kernel(
             if j % 2 == 0 and j >= 2:
                 deps += ["OUT_%d" % (j - 1), "OUT_%d" % (j - 2)]
             unit("S2_%d" % j, ("pe",), 111, base - 32, deps, emit_s2, kind="m")
-            unit("OUT_%d" % j, ("dve",), 300, base - 31, ["S2_%d" % j, "EVB%d" % (j // 4), "EVB%d" % (2 + j // 4)], emit_out)
+            unit("OUT_%d" % j, ("dve",), 300, base - 31, ["S2_%d" % j, "bias3"], emit_out)
 
         for name, eng, bank in plan(units, names, landed):
             units[name]["emit"](eng, bank)

@@ -18,11 +18,11 @@ OUT = 128
 FLOPS = 2 * 128 * NM * (2 * 512 * 512 + 2 * 512 * 128)
 
 N_TP = 4
+N_LS = 1
 N_G2 = 6
 N_C2 = 6
 N_G3 = 4
-N_JUNK = 2
-HOP = 80.0
+HOP = 400.0
 SWITCH = 90.0
 
 
@@ -134,7 +134,7 @@ def tile_skill_net_pb_kernel(
 
         def load_w2(j):
             for m in (1, 0):
-                nc.sync.dma_start(out=w2_sb[m][j][:], in_=w2_dram[m][j].rearrange("(p c) k -> p c k", c=4))
+                nc.sync.dma_start(out=w2_sb[m][j][:].rearrange("p (u e) k -> p u (e k)", u=2), in_=w2_dram[m][j].rearrange("(u p e) k -> p u (e k)", u=2, e=2))
                 lands("w2_%d_%d" % (m, j), 512)
 
         def load_w3(q):
@@ -154,18 +154,18 @@ def tile_skill_net_pb_kernel(
         load_w2(0)
         load_w2(1)
         load_x1(1)
-        load_w3(0)
         load_w2(2)
-        load_bias3()
         load_w2(3)
         load_x1(2)
-        load_w3(1)
         load_w2(4)
         load_w2(5)
         load_x1(3)
-        load_w3(2)
         load_w2(6)
         load_w2(7)
+        load_bias3()
+        load_w3(0)
+        load_w3(1)
+        load_w3(2)
         load_w3(3)
 
         units = {}
@@ -207,9 +207,9 @@ def tile_skill_net_pb_kernel(
 
         def emit_tr(eng, bank):
             rt = new_bank("TR", bank)
-            rows_w = rows[:].bitcast(F32).rearrange("r (q u) -> r q u", u=2)
+            rows_w = rows[:].bitcast(F32)
             for u in range(2):
-                nc.tensor.transpose(rt[:, u, :], rows_w[:, :, u], ident[:])
+                nc.tensor.transpose(rt[:, u, :], rows_w[:, P * u : P * u + P], ident[:])
 
         def emit_evr(eng, bank):
             nc.vector.tensor_copy(
@@ -232,7 +232,7 @@ def tile_skill_net_pb_kernel(
             )
             nc.vector.tensor_copy(out=bias12[:].rearrange("p m j c -> p (m j c)"), in_=vec_bf[:, 32:96])
 
-        unit("TR", ("pe",), 210, -100, ["small"], emit_tr, bank="take", kind="t")
+        unit("TR", ("pe",), 130, -100, ["small"], emit_tr, bank="take", kind="t")
         unit("EVR", ("dve",), 100, -100, ["TR"], emit_evr, bank="TR")
         unit("chain", ("dve",), 260, -99, ["EVR"], emit_chain)
         unit("sign", ("dve",), 200, -98, ["chain"], emit_sign)
@@ -259,7 +259,7 @@ def tile_skill_net_pb_kernel(
             def emit_evfi(eng, bank, h=h):
                 copy_out(eng, fi_all[:, 4 * h : 4 * h + 4, :], banks["TFI%d" % h][:])
 
-            unit("TFI%d" % h, ("pe",), 260, -40 + 245 * h, ["fac0"], emit_tfi, bank="take", kind="t")
+            unit("TFI%d" % h, ("pe",), 420, -40 + 245 * h, ["fac0"], emit_tfi, bank="take", kind="t")
             unit("EVFI%d" % h, ("act", "dve"), 445, -40 + 245 * h, ["TFI%d" % h], emit_evfi, bank="TFI%d" % h)
 
         x1_g = work.tile([P, NM * K], BF16, name="x1_g", align_bytes=64)
@@ -290,7 +290,7 @@ def tile_skill_net_pb_kernel(
                 )
 
             pr = 200 * q - 60
-            unit("TX%d" % q, ("pe",), 260, pr, ["x1_%d" % q], emit_tx, bank="take", kind="t")
+            unit("TX%d" % q, ("pe",), 420, pr, ["x1_%d" % q], emit_tx, bank="take", kind="t")
             unit("EVX%d" % q, ("act", "dve"), 445, pr, ["TX%d" % q], emit_evx, bank="TX%d" % q, after=100.0)
             unit("QX%d" % q, ("dve",), 240, pr, ["EVX%d" % q], emit_qx, after=100.0)
 
@@ -332,7 +332,7 @@ def tile_skill_net_pb_kernel(
                     deps = [tn]
                     if idx >= N_G2:
                         deps.append("Q%d_%d" % (1 - (idx - N_G2) % 2, (idx - N_G2) // 2))
-                    unit(tn, ("pe",), 260, base - 50 + off + hf, ["w2_%d_%d" % (m, j)], emit_t2, bank="take", kind="t")
+                    unit(tn, ("pe",), 420, base - 50 + off + hf, ["w2_%d_%d" % (m, j)], emit_t2, bank="take", kind="t")
                     unit("EV%d_%d_%d" % (m, j, hf), ("act", "dve"), 445, base - 50 + off + hf, deps, emit_ev2, bank=tn, after=100.0)
 
                 def emit_q2(eng, bank, j=j, m=m, idx=idx):
@@ -349,19 +349,9 @@ def tile_skill_net_pb_kernel(
                 def emit_s1(eng, bank, j=j, m=m):
                     codes, scales = q2[(j, m)]
                     if m == 1:
-                        ps = psum.tile([P, 4, P], F32, name="ps_ls", tag="ls")
+                        ps = psum.tile([P, 4, P], F32, name="ps_ls", tag="ls%d" % (j % N_LS))
                     else:
                         ps = psum.tile([P, 4, P], F32, name="ps_mu", tag="mu%d" % (j % 2))
-                    for rep in range(N_JUNK):
-                        nc.tensor.matmul_mx(
-                            out=ps[:].rearrange("p c b -> p (c b)"),
-                            lhsT=codes[:, 0:P].bitcast(FP8X4),
-                            lhsT_scale=scales[:, 0:P],
-                            rhs=codes[:].bitcast(FP8X4),
-                            rhs_scale=scales[:],
-                            start=True,
-                            stop=True,
-                        )
                     for c in range(4):
                         nc.tensor.matmul_mx(
                             out=ps[:, c, :],
@@ -375,8 +365,8 @@ def tile_skill_net_pb_kernel(
                     acc[(j, m)] = ps
 
                 deps = ["Q%d_%d" % (m, j), "QX%d" % (j // 2)]
-                if m == 1 and j >= 1:
-                    deps.append("a_%d" % (j - 1))
+                if m == 1 and j >= N_LS:
+                    deps.append("a_%d" % (j - N_LS))
                 if m == 0 and j >= 2:
                     deps.append("d_%d" % (j - 2))
                 unit("S1_%d_%d" % (m, j), ("pe",), 250, base - 40 + (1 - m), deps, emit_s1, kind="m")
@@ -384,9 +374,9 @@ def tile_skill_net_pb_kernel(
             def emit_t3(eng, bank, j=j):
                 xt = new_bank("TW3_%d" % j, bank)
                 for m in range(2):
-                    words = w3_sb[m][j // 2][:, j % 2, :].bitcast(F32).rearrange("o (q u) -> o q u", u=2)
+                    words = w3_sb[m][j // 2][:, j % 2, :].bitcast(F32)
                     for u in range(2):
-                        nc.tensor.transpose(xt[:, 2 * m + u, :], words[:, :, u], ident[:])
+                        nc.tensor.transpose(xt[:, 2 * m + u, :], words[:, P * u : P * u + P], ident[:])
 
             def emit_ev3(eng, bank, j=j):
                 g3[j] = work.tile([P, 2 * K], BF16, name="w3_g", tag="w3_g%d" % (j % N_G3), align_bytes=64)
@@ -405,7 +395,7 @@ def tile_skill_net_pb_kernel(
             deps = ["TW3_%d" % j]
             if j >= N_G3:
                 deps.append("QW3_%d" % (j - N_G3))
-            unit("TW3_%d" % j, ("pe",), 416, base - 20, ["w3_%d" % (j // 2)], emit_t3, bank="take", kind="t")
+            unit("TW3_%d" % j, ("pe",), 420, base - 20, ["w3_%d" % (j // 2)], emit_t3, bank="take", kind="t")
             unit("EVW3_%d" % j, ("act", "dve"), 445, base - 20, deps, emit_ev3, bank="TW3_%d" % j, after=100.0)
             unit("QW3_%d" % j, ("dve",), 240, base - 20, ["EVW3_%d" % j], emit_q3, after=100.0)
 
@@ -536,8 +526,10 @@ def tile_skill_net_pb_kernel(
             deps = ["qx2_%d" % j, "QW3_%d" % j]
             if j % 2 == 0 and j >= 2:
                 deps += ["OUT_%d" % (j - 1), "OUT_%d" % (j - 2)]
+            if j % 2 == 1:
+                deps.append("S2_%d" % (j - 1))
             unit("S2_%d" % j, ("pe",), 111, base - 32, deps, emit_s2, kind="m")
-            unit("OUT_%d" % j, ("dve",), 300, base - 31, ["S2_%d" % j, "bias3"], emit_out)
+            unit("OUT_%d" % j, ("dve",), 300, base - 31, ["S2_%d" % j, "bias3"] + (older("OUT_%d", 1) if j % 2 == 1 else []), emit_out)
 
         for name, eng, bank in plan(units, names, landed):
             units[name]["emit"](eng, bank)

@@ -19,10 +19,13 @@ FLOPS = 2 * 128 * NM * (2 * 512 * 512 + 2 * 512 * 128)
 
 N_TP = 4
 N_LS = 1
+N_MU = 2
 N_G2 = 6
 N_C2 = 6
 N_G3 = 4
-HOP = 400.0
+LAG = {"pe": 400.0, "act": 200.0, "dve": 200.0, "pool": 300.0}
+SAME = 200.0
+LANDING = 100.0
 SWITCH = 90.0
 
 
@@ -46,9 +49,11 @@ def plan(units, names, landed):
             for eng in u["engines"]:
                 t = 0.0
                 for d in u["deps"]:
-                    lag = 0.0 if where.get(d, "") == eng else HOP
+                    lag = LANDING
                     if d in units:
-                        lag += units[d]["after"]
+                        lag = LAG[where[d]]
+                        if where[d] == eng:
+                            lag = 0.0 if (eng == "pe" or units[d]["quick"]) else SAME
                     t = max(t, done[d] + lag)
                 bank = -1
                 if u["bank"] == "take":
@@ -56,7 +61,7 @@ def plan(units, names, landed):
                     if not cands:
                         continue
                     bank = min(cands, key=lambda s: bank_free[s])
-                    t = max(t, bank_free[bank] + HOP)
+                    t = max(t, bank_free[bank])
                 start = max(t, free[eng])
                 key = (start, u["prio"])
                 if best is None or key < best[0]:
@@ -79,7 +84,7 @@ def plan(units, names, landed):
         if u["bank"] != "" and u["bank"] != "take":
             b = bank_of[u["bank"]]
             bank_open[b] = True
-            bank_free[b] = end
+            bank_free[b] = end + LAG[eng]
         todo = [n for n in todo if n != name]
         seq.append((name, eng, bank))
     return seq
@@ -172,7 +177,7 @@ def tile_skill_net_pb_kernel(
         names = []
         banks = {}
 
-        def unit(name, engines, cost, prio, deps, emit, bank="", kind="", after=0.0):
+        def unit(name, engines, cost, prio, deps, emit, bank="", kind="", quick=False):
             units[name] = {
                 "engines": engines,
                 "cost": cost,
@@ -181,7 +186,7 @@ def tile_skill_net_pb_kernel(
                 "emit": emit,
                 "bank": bank,
                 "kind": kind,
-                "after": after,
+                "quick": quick,
             }
             names.append(name)
 
@@ -220,22 +225,22 @@ def tile_skill_net_pb_kernel(
         def emit_chain(eng, bank):
             nc.vector.tensor_copy(out=noise_in[:, 0:8], in_=ei_sb[:])
             nc.vector.tensor_copy(out=noise_in[:, 8:40], in_=vec_bf[:, 0:32])
+            nc.vector.tensor_copy(out=bias12[:].rearrange("p m j c -> p (m j c)"), in_=vec_bf[:, 32:96])
             nc.vector.scalar_tensor_tensor(
                 out=mag[:], in0=noise_in[:], scalar=-1.0, in1=noise_in[:], op0=ALU.mult, op1=ALU.max
             )
+            nc.vector.tensor_single_scalar(out=neg[:], in_=noise_in[:], scalar=0.0, op=ALU.is_lt)
             nc.vector.tensor_scalar_max(out=mag[:], in0=mag[:], scalar1=2.0 ** -116)
 
         def emit_sign(eng, bank):
-            nc.vector.tensor_single_scalar(out=neg[:], in_=noise_in[:], scalar=0.0, op=ALU.is_lt)
             nc.vector.scalar_tensor_tensor(
                 out=sgn[:], in0=noise_in[:], scalar=0.0, in1=neg[:], op0=ALU.is_gt, op1=ALU.subtract
             )
-            nc.vector.tensor_copy(out=bias12[:].rearrange("p m j c -> p (m j c)"), in_=vec_bf[:, 32:96])
 
         unit("TR", ("pe",), 130, -100, ["small"], emit_tr, bank="take", kind="t")
         unit("EVR", ("dve",), 100, -100, ["TR"], emit_evr, bank="TR")
-        unit("chain", ("dve",), 260, -99, ["EVR"], emit_chain)
-        unit("sign", ("dve",), 200, -98, ["chain"], emit_sign)
+        unit("chain", ("dve",), 700, -99, ["EVR"], emit_chain)
+        unit("sign", ("dve",), 70, -98, ["chain"], emit_sign, quick=True)
         pieces = ((0, 8), (8, 12), (12, 16), (16, 24), (24, 40))
         for i, (lo, hi) in enumerate(pieces):
 
@@ -259,7 +264,7 @@ def tile_skill_net_pb_kernel(
             def emit_evfi(eng, bank, h=h):
                 copy_out(eng, fi_all[:, 4 * h : 4 * h + 4, :], banks["TFI%d" % h][:])
 
-            unit("TFI%d" % h, ("pe",), 420, -40 + 245 * h, ["fac0"], emit_tfi, bank="take", kind="t")
+            unit("TFI%d" % h, ("pe",), 300, -40 + 245 * h, ["fac0"], emit_tfi, bank="take", kind="t")
             unit("EVFI%d" % h, ("act", "dve"), 445, -40 + 245 * h, ["TFI%d" % h], emit_evfi, bank="TFI%d" % h)
 
         x1_g = work.tile([P, NM * K], BF16, name="x1_g", align_bytes=64)
@@ -290,9 +295,9 @@ def tile_skill_net_pb_kernel(
                 )
 
             pr = 200 * q - 60
-            unit("TX%d" % q, ("pe",), 420, pr, ["x1_%d" % q], emit_tx, bank="take", kind="t")
-            unit("EVX%d" % q, ("act", "dve"), 445, pr, ["TX%d" % q], emit_evx, bank="TX%d" % q, after=100.0)
-            unit("QX%d" % q, ("dve",), 240, pr, ["EVX%d" % q], emit_qx, after=100.0)
+            unit("TX%d" % q, ("pe",), 300, pr, ["x1_%d" % q], emit_tx, bank="take", kind="t")
+            unit("EVX%d" % q, ("act", "dve"), 445, pr, ["TX%d" % q], emit_evx, bank="TX%d" % q)
+            unit("QX%d" % q, ("dve",), 240, pr, ["EVX%d" % q], emit_qx)
 
         g2 = {}
         q2 = {}
@@ -332,8 +337,8 @@ def tile_skill_net_pb_kernel(
                     deps = [tn]
                     if idx >= N_G2:
                         deps.append("Q%d_%d" % (1 - (idx - N_G2) % 2, (idx - N_G2) // 2))
-                    unit(tn, ("pe",), 420, base - 50 + off + hf, ["w2_%d_%d" % (m, j)], emit_t2, bank="take", kind="t")
-                    unit("EV%d_%d_%d" % (m, j, hf), ("act", "dve"), 445, base - 50 + off + hf, deps, emit_ev2, bank=tn, after=100.0)
+                    unit(tn, ("pe",), 300, base - 50 + off + hf, ["w2_%d_%d" % (m, j)], emit_t2, bank="take", kind="t")
+                    unit("EV%d_%d_%d" % (m, j, hf), ("act", "dve"), 445, base - 50 + off + hf, deps, emit_ev2, bank=tn)
 
                 def emit_q2(eng, bank, j=j, m=m, idx=idx):
                     codes = work.tile([P, K], U32, name="w2_c", tag="w2_c%d" % (idx % N_C2), align_bytes=64)
@@ -344,14 +349,14 @@ def tile_skill_net_pb_kernel(
                 deps = ["EV%d_%d_0" % (m, j), "EV%d_%d_1" % (m, j)]
                 if idx >= N_C2:
                     deps.append("S1_%d_%d" % (1 - (idx - N_C2) % 2, (idx - N_C2) // 2))
-                unit("Q%d_%d" % (m, j), ("dve",), 477, base - 50 + off + 2, deps, emit_q2, after=100.0)
+                unit("Q%d_%d" % (m, j), ("dve",), 477, base - 50 + off + 2, deps, emit_q2)
 
                 def emit_s1(eng, bank, j=j, m=m):
                     codes, scales = q2[(j, m)]
                     if m == 1:
                         ps = psum.tile([P, 4, P], F32, name="ps_ls", tag="ls%d" % (j % N_LS))
                     else:
-                        ps = psum.tile([P, 4, P], F32, name="ps_mu", tag="mu%d" % (j % 2))
+                        ps = psum.tile([P, 4, P], F32, name="ps_mu", tag="mu%d" % (j % N_MU))
                     for c in range(4):
                         nc.tensor.matmul_mx(
                             out=ps[:, c, :],
@@ -367,8 +372,8 @@ def tile_skill_net_pb_kernel(
                 deps = ["Q%d_%d" % (m, j), "QX%d" % (j // 2)]
                 if m == 1 and j >= N_LS:
                     deps.append("a_%d" % (j - N_LS))
-                if m == 0 and j >= 2:
-                    deps.append("d_%d" % (j - 2))
+                if m == 0 and j >= N_MU:
+                    deps.append("d_%d" % (j - N_MU))
                 unit("S1_%d_%d" % (m, j), ("pe",), 250, base - 40 + (1 - m), deps, emit_s1, kind="m")
 
             def emit_t3(eng, bank, j=j):
@@ -395,9 +400,9 @@ def tile_skill_net_pb_kernel(
             deps = ["TW3_%d" % j]
             if j >= N_G3:
                 deps.append("QW3_%d" % (j - N_G3))
-            unit("TW3_%d" % j, ("pe",), 420, base - 20, ["w3_%d" % (j // 2)], emit_t3, bank="take", kind="t")
-            unit("EVW3_%d" % j, ("act", "dve"), 445, base - 20, deps, emit_ev3, bank="TW3_%d" % j, after=100.0)
-            unit("QW3_%d" % j, ("dve",), 240, base - 20, ["EVW3_%d" % j], emit_q3, after=100.0)
+            unit("TW3_%d" % j, ("pe",), 300, base - 20, ["w3_%d" % (j // 2)], emit_t3, bank="take", kind="t")
+            unit("EVW3_%d" % j, ("act", "dve"), 445, base - 20, deps, emit_ev3, bank="TW3_%d" % j)
+            unit("QW3_%d" % j, ("dve",), 240, base - 20, ["EVW3_%d" % j], emit_q3)
 
             def emit_a(eng, bank, j=j):
                 e = work.tile([P, 4, P], F32, name="e", tag="e%d" % (j % 2))
@@ -497,20 +502,29 @@ def tile_skill_net_pb_kernel(
                     in1=bias3[:, j].rearrange("p m o -> p (m o)"),
                     op=ALU.add,
                 )
-                nc.vector.tensor_scalar(
-                    out=r[:, j % 2, 1, :], in0=r[:, j % 2, 1, :], scalar1=-20.0, scalar2=2.0, op0=ALU.max, op1=ALU.min
-                )
                 if q == 3:
                     nc.sync.dma_start(out=out_0[:, j, :], in_=r[:, j % 2, 0, :])
-                    nc.sync.dma_start(out=out_1[:, j, :], in_=r[:, j % 2, 1, :])
                 elif j % 2 == 1:
                     nc.sync.dma_start(out=out_0[:, 2 * q : 2 * q + 2, :], in_=r[:, :, 0, :])
+
+            def emit_clip(eng, bank, j=j):
+                q = j // 2
+                r = res[q]
+                if q == 3:
+                    nc.vector.tensor_scalar(
+                        out=r[:, j % 2, 1, :], in0=r[:, j % 2, 1, :], scalar1=-20.0, scalar2=2.0, op0=ALU.max, op1=ALU.min
+                    )
+                    nc.sync.dma_start(out=out_1[:, j, :], in_=r[:, j % 2, 1, :])
+                else:
+                    nc.vector.tensor_scalar(
+                        out=r[:, :, 1, :], in0=r[:, :, 1, :], scalar1=-20.0, scalar2=2.0, op0=ALU.max, op1=ALU.min
+                    )
                     nc.sync.dma_start(out=out_1[:, 2 * q : 2 * q + 2, :], in_=r[:, :, 1, :])
 
             def older(name, back):
                 return [name % (j - back)] if j >= back else []
 
-            unit("a_%d" % j, ("act",), 600, base - 38, ["S1_1_%d" % j, "sign"] + older("b_%d", 2), emit_a)
+            unit("a_%d" % j, ("act",), 600, base - 38, ["S1_1_%d" % j, "chain"] + older("b_%d", 2), emit_a)
             unit("b_%d" % j, ("dve",), 226, base - 37, ["a_%d" % j] + older("c_%d", 2), emit_b)
             unit(
                 "c_%d" % j,
@@ -519,17 +533,22 @@ def tile_skill_net_pb_kernel(
                 base - 36,
                 ["b_%d" % j, "EVFI%d" % (j // 4), "fac%d" % (1 + min(j, 2) + (j // 4))] + older("d_%d", 2),
                 emit_c,
+                quick=True,
             )
             unit("d_%d" % j, ("dve",), 480, base - 35, ["c_%d" % j, "S1_0_%d" % j] + older("e_%d", 2), emit_d)
             unit("e_%d" % j, ("act",), 550, base - 34, ["d_%d" % j] + older("qx2_%d", 2), emit_e)
-            unit("qx2_%d" % j, ("dve",), 140, base - 33, ["e_%d" % j], emit_qx2, after=150.0)
+            unit("qx2_%d" % j, ("dve",), 140, base - 33, ["e_%d" % j], emit_qx2)
             deps = ["qx2_%d" % j, "QW3_%d" % j]
             if j % 2 == 0 and j >= 2:
                 deps += ["OUT_%d" % (j - 1), "OUT_%d" % (j - 2)]
             if j % 2 == 1:
                 deps.append("S2_%d" % (j - 1))
             unit("S2_%d" % j, ("pe",), 111, base - 32, deps, emit_s2, kind="m")
-            unit("OUT_%d" % j, ("dve",), 300, base - 31, ["S2_%d" % j, "bias3"] + (older("OUT_%d", 1) if j % 2 == 1 else []), emit_out)
+            unit("OUT_%d" % j, ("dve",), 230, base - 31, ["S2_%d" % j, "bias3"] + (older("OUT_%d", 1) if j % 2 == 1 else []), emit_out)
+            if j >= 6:
+                unit("CLIP_%d" % j, ("dve",), 70, base - 30, ["OUT_%d" % j], emit_clip)
+            elif j % 2 == 1:
+                unit("CLIP_%d" % j, ("dve",), 125, base - 30, ["OUT_%d" % j], emit_clip)
 
         for name, eng, bank in plan(units, names, landed):
             units[name]["emit"](eng, bank)

@@ -14,80 +14,10 @@ ACT = mybir.ActivationFunctionType
 P = 128
 NM = 8
 K = 512
-OUT = 128
-FLOPS = 2 * 128 * NM * (2 * 512 * 512 + 2 * 512 * 128)
-
-N_TP = 4
-N_LS = 1
-N_MU = 2
-N_G2 = 6
-N_C2 = 6
-N_G3 = 4
-LAG = {"pe": 400.0, "act": 200.0, "dve": 200.0, "pool": 300.0}
-SAME = 200.0
-LANDING = 100.0
-SWITCH = 90.0
-
-
-def plan(units, names, landed):
-    done = dict(landed)
-    where = {}
-    free = {"pe": 0.0, "act": 0.0, "dve": 0.0, "pool": 0.0}
-    bank_free = [0.0] * N_TP
-    bank_open = [True] * N_TP
-    bank_of = {}
-    todo = list(names)
-    seq = []
-    kind = [""]
-    while todo:
-        best = None
-        for name in todo:
-            u = units[name]
-            ready = all(d in done for d in u["deps"])
-            if not ready:
-                continue
-            for eng in u["engines"]:
-                t = 0.0
-                for d in u["deps"]:
-                    lag = LANDING
-                    if d in units:
-                        lag = LAG[where[d]]
-                        if where[d] == eng:
-                            lag = 0.0 if (eng == "pe" or units[d]["quick"]) else SAME
-                    t = max(t, done[d] + lag)
-                bank = -1
-                if u["bank"] == "take":
-                    cands = [s for s in range(N_TP) if bank_open[s]]
-                    if not cands:
-                        continue
-                    bank = min(cands, key=lambda s: bank_free[s])
-                    t = max(t, bank_free[bank])
-                start = max(t, free[eng])
-                key = (start, u["prio"])
-                if best is None or key < best[0]:
-                    best = (key, name, eng, bank)
-        assert best is not None, "the plan is stuck"
-        key, name, eng, bank = best
-        u = units[name]
-        cost = u["cost"]
-        if eng == "pe":
-            if kind[0] != "" and kind[0] != u["kind"]:
-                cost += SWITCH
-            kind[0] = u["kind"]
-        end = key[0] + cost
-        done[name] = end
-        where[name] = eng
-        free[eng] = end
-        if bank >= 0:
-            bank_open[bank] = False
-            bank_of[name] = bank
-        if u["bank"] != "" and u["bank"] != "take":
-            b = bank_of[u["bank"]]
-            bank_open[b] = True
-            bank_free[b] = end + LAG[eng]
-        todo = [n for n in todo if n != name]
-        seq.append((name, eng, bank))
-    return seq
+CHUNKS = 4
+MU, LS = 0, 1
+N_BANKS = 5
+FLOPS = 2 * P * NM * (2 * K * K + 2 * K * P)
 
 
 def tile_skill_net_pb_kernel(
@@ -96,16 +26,12 @@ def tile_skill_net_pb_kernel(
     nc = tc.nc
     with ExitStack() as ctx:
         ctx.enter_context(tc.manual_schedule())
-        const = ctx.enter_context(tc.tile_pool(name="const", bufs=1))
-        raw = ctx.enter_context(tc.tile_pool(name="raw", bufs=1))
-        work = ctx.enter_context(tc.tile_pool(name="work", bufs=1))
+        keep = ctx.enter_context(tc.tile_pool(name="keep", bufs=1))
+        turn = ctx.enter_context(tc.tile_pool(name="turn", bufs=2))
         psum = ctx.enter_context(tc.psum_pool(name="psum", bufs=1))
 
-        clip_in = const.tile([P, 2], F32, name="clip_in")
-        nc.vector.memset(clip_in[:, 0:1], -20.0)
-        nc.vector.memset(clip_in[:, 1:2], 4.0)
-        rows = const.tile([P, K], BF16, name="rows")
-        ei_sb = const.tile([P, NM], BF16, name="ei_sb")
+        rows = keep.tile([P, K], BF16, name="rows")
+        ei_sb = keep.tile([P, NM], BF16, name="ei_sb")
         nc.scalar.dma_start(out=ei_sb[:], in_=ei2.rearrange("b j o -> b (j o)"))
         nc.scalar.dma_start(out=rows[0:8, :], in_=ej2.rearrange("o j h -> (o j) h"))
         nc.scalar.dma_start(out=rows[8:16, :], in_=b21)
@@ -113,442 +39,323 @@ def tile_skill_net_pb_kernel(
         nc.scalar.dma_start(out=rows[24:32, :], in_=b22)
         nc.vector.memset(rows[32:64, :], 0.0)
         nc.vector.memset(rows[64:128, :], 0.0)
-        half = const.tile([P, 40], F32, name="half")
-        nc.vector.memset(half[:], 0.5)
-        clip_e = const.tile([P, 2], F32, name="clip_e")
+        clip_in = keep.tile([P, 2], F32, name="clip_in")
+        nc.vector.memset(clip_in[:, 0:1], -20.0)
+        nc.vector.memset(clip_in[:, 1:2], 4.0)
+        clip_e = keep.tile([P, 2], F32, name="clip_e")
         nc.scalar.activation(out=clip_e[:], in_=clip_in[:], func=ACT.Exp)
-        ident = const.tile([P, P], F32, name="ident")
+        half = keep.tile([P, 8 + CHUNKS * NM], F32, name="half")
+        nc.vector.memset(half[:], 0.5)
+        ident = keep.tile([P, P], F32, name="ident")
         make_identity(nc, ident[:])
 
-        x1_sb = [raw.tile([P, 2, K], BF16, name="x1_sb%d" % q) for q in range(4)]
-        w2_sb = [[raw.tile([P, 4, K], BF16, name="w2_sb%d_%d" % (m, j)) for j in range(NM)] for m in range(2)]
-        w3_sb = [[raw.tile([P, 2, K], BF16, name="w3_sb%d_%d" % (m, q)) for q in range(4)] for m in range(2)]
-        bias3 = const.tile([P, NM, 2, OUT], BF16, name="bias3")
-        w2_dram = (w21, w22)
-        w3_dram = (w31, w32)
-        landed = {}
-        clock = [2000.0]
-
-        def lands(name, kib):
-            clock[0] += kib / 0.56
-            landed[name] = clock[0]
-
-        def load_x1(q):
-            nc.sync.dma_start(out=x1_sb[q][:], in_=x1[:, 2 * q : 2 * q + 2, :])
-            lands("x1_%d" % q, 256)
-
-        def load_w2(j):
-            for m in (1, 0):
-                nc.sync.dma_start(out=w2_sb[m][j][:].rearrange("p (u e) k -> p u (e k)", u=2), in_=w2_dram[m][j].rearrange("(u p e) k -> p u (e k)", u=2, e=2))
-                lands("w2_%d_%d" % (m, j), 512)
-
-        def load_w3(q):
-            for m in range(2):
+        x1_sb = [keep.tile([P, 4, K], BF16, name="x1_sb%d" % h) for h in range(2)]
+        w2_sb = [[keep.tile([P, CHUNKS, K], BF16, name="w2_sb%d_%d" % (m, j)) for j in range(NM)] for m in range(2)]
+        w3_sb = [[keep.tile([P, 2, K], BF16, name="w3_sb%d_%d" % (m, q)) for q in range(NM // 2)] for m in range(2)]
+        bias3 = keep.tile([P, NM, 2, P], BF16, name="bias3")
+        for h in range(2):
+            nc.sync.dma_start(out=x1_sb[h][:], in_=x1[:, 4 * h : 4 * h + 4, :])
+        for j in range(NM):
+            for m, w in ((LS, w22), (MU, w21)):
                 nc.sync.dma_start(
-                    out=w3_sb[m][q][:], in_=w3_dram[m][2 * q : 2 * q + 2].rearrange("j o h -> o j h")
+                    out=w2_sb[m][j][:].rearrange("p (u e) k -> p u (e k)", u=2),
+                    in_=w[j].rearrange("(u p e) k -> p u (e k)", u=2, e=2),
                 )
-            lands("w3_%d" % q, 512)
+            if j % 2 == 1:
+                q = j // 2
+                for m, w in ((0, w31), (1, w32)):
+                    nc.sync.dma_start(out=w3_sb[m][q][:], in_=w[2 * q : 2 * q + 2].rearrange("j o h -> o j h"))
+        nc.sync.dma_start(out=bias3[:, :, 0, :], in_=b31.partition_broadcast(P))
+        nc.sync.dma_start(out=bias3[:, :, 1, :], in_=b32.partition_broadcast(P))
 
-        def load_bias3():
-            nc.sync.dma_start(out=bias3[:, :, 0, :], in_=b31.partition_broadcast(P))
-            nc.sync.dma_start(out=bias3[:, :, 1, :], in_=b32.partition_broadcast(P))
-            lands("bias3", 512)
+        banks_used = [0]
+        bank_of = {}
 
-        landed["small"] = 3000.0
-        load_x1(0)
-        load_w2(0)
-        load_w2(1)
-        load_x1(1)
-        load_w2(2)
-        load_w2(3)
-        load_x1(2)
-        load_w2(4)
-        load_w2(5)
-        load_x1(3)
-        load_w2(6)
-        load_w2(7)
-        load_bias3()
-        load_w3(0)
-        load_w3(1)
-        load_w3(2)
-        load_w3(3)
+        def next_bank(key):
+            bank_of[key] = psum.tile([P, 4, P], F32, name="bank", tag="bank%d" % (banks_used[0] % N_BANKS))
+            banks_used[0] += 1
+            return bank_of[key]
 
-        units = {}
-        names = []
-        banks = {}
+        def transpose_words(key, sources):
+            bank = next_bank(key)
+            for i, words in enumerate(sources):
+                nc.tensor.transpose(bank[:, i, :], words, ident[:])
 
-        def unit(name, engines, cost, prio, deps, emit, bank="", kind="", quick=False):
-            units[name] = {
-                "engines": engines,
-                "cost": cost,
-                "prio": prio,
-                "deps": deps,
-                "emit": emit,
-                "bank": bank,
-                "kind": kind,
-                "quick": quick,
-            }
-            names.append(name)
+        def halves(tile_2d):
+            words = tile_2d.bitcast(F32)
+            return [words[:, 0:P], words[:, P : 2 * P]]
 
-        def copy_out(eng, out, in_):
-            if eng == "act":
+        def regroup(engine, key, grouped):
+            out = grouped.bitcast(F32).rearrange("p (i c u) -> p i c u", i=2, u=2)
+            in_ = bank_of[key][:].rearrange("p (i u) c -> p i c u", u=2)
+            if engine == "scalar":
                 nc.scalar.copy(out=out, in_=in_)
             else:
                 nc.vector.tensor_copy(out=out, in_=in_)
 
-        def new_bank(name, bank):
-            banks[name] = psum.tile([P, 4, P], F32, name="tp", tag="tp%d" % bank)
-            return banks[name]
+        def quantise(grouped, name, pool):
+            width = grouped.shape[1] // 4
+            codes = pool.tile([P, width], U32, name=name + "_c", align_bytes=64)
+            scales = pool.tile([P, width], U8, name=name + "_s", align_bytes=64)
+            nc.vector.quantize_mx(out=codes[:].bitcast(FP8X4), scales=scales[:], in_=grouped)
+            return codes, scales
 
-        vec_bf = const.tile([P, 96], BF16, name="vec_bf")
-        noise_in = const.tile([P, 40], F32, name="noise_in")
-        bias12 = const.tile([P, 2, NM, 4], F32, name="bias12")
-        mag = const.tile([P, 40], F32, name="mag")
-        neg = const.tile([P, 40], F32, name="neg")
-        sgn = const.tile([P, 40], F32, name="sgn")
-        root = const.tile([P, 40], F32, name="root")
-        fac = const.tile([P, 40], F32, name="fac")
-        fi_all = const.tile([P, NM, P], F32, name="fi_all")
+        def pass_mx(out, stationary, moving, s_cols, m_cols):
+            nc.tensor.matmul_mx(
+                out=out,
+                lhsT=stationary[0][:, s_cols].bitcast(FP8X4),
+                lhsT_scale=stationary[1][:, s_cols],
+                rhs=moving[0][:, m_cols].bitcast(FP8X4),
+                rhs_scale=moving[1][:, m_cols],
+                start=True,
+                stop=True,
+            )
 
-        def emit_tr(eng, bank):
-            rt = new_bank("TR", bank)
-            rows_w = rows[:].bitcast(F32)
-            for u in range(2):
-                nc.tensor.transpose(rt[:, u, :], rows_w[:, P * u : P * u + P], ident[:])
+        vec = keep.tile([P, 24 * CHUNKS], BF16, name="vec")
+        draws = keep.tile([P, 8 + CHUNKS * NM], F32, name="draws")
+        bias12 = keep.tile([P, 2, NM, CHUNKS], F32, name="bias12")
+        mag = keep.tile([P, 8 + CHUNKS * NM], F32, name="mag")
+        neg = keep.tile([P, 8 + CHUNKS * NM], F32, name="neg")
+        sgn = keep.tile([P, 8 + CHUNKS * NM], F32, name="sgn")
+        root = keep.tile([P, 8 + CHUNKS * NM], F32, name="root")
+        fac = keep.tile([P, 8 + CHUNKS * NM], F32, name="fac")
+        row_fac = keep.tile([P, NM, P], F32, name="row_fac")
 
-        def emit_evr(eng, bank):
+        def small_vectors():
+            bank = next_bank("rows")
+            for u, words in enumerate(halves(rows[:])):
+                nc.tensor.transpose(bank[:, u, :], words, ident[:])
             nc.vector.tensor_copy(
-                out=vec_bf[:].bitcast(F32).rearrange("p (r u) -> p r u", u=2),
-                in_=banks["TR"][:, 0:2, 0:24].rearrange("p u r -> p r u"),
+                out=vec[:].bitcast(F32).rearrange("p (r u) -> p r u", u=2),
+                in_=bank[:, 0:2, 0:24].rearrange("p u r -> p r u"),
             )
-
-        def emit_chain(eng, bank):
-            nc.vector.tensor_copy(out=noise_in[:, 0:8], in_=ei_sb[:])
-            nc.vector.tensor_copy(out=noise_in[:, 8:40], in_=vec_bf[:, 0:32])
-            nc.vector.tensor_copy(out=bias12[:].rearrange("p m j c -> p (m j c)"), in_=vec_bf[:, 32:96])
+            nc.vector.tensor_copy(out=draws[:, 0:8], in_=ei_sb[:])
+            nc.vector.tensor_copy(out=draws[:, 8:], in_=vec[:, 0 : CHUNKS * NM])
+            nc.vector.tensor_copy(out=bias12[:].rearrange("p m j c -> p (m j c)"), in_=vec[:, CHUNKS * NM :])
             nc.vector.scalar_tensor_tensor(
-                out=mag[:], in0=noise_in[:], scalar=-1.0, in1=noise_in[:], op0=ALU.mult, op1=ALU.max
+                out=mag[:], in0=draws[:], scalar=-1.0, in1=draws[:], op0=ALU.mult, op1=ALU.max
             )
-            nc.vector.tensor_single_scalar(out=neg[:], in_=noise_in[:], scalar=0.0, op=ALU.is_lt)
+            nc.vector.tensor_single_scalar(out=neg[:], in_=draws[:], scalar=0.0, op=ALU.is_lt)
             nc.vector.tensor_scalar_max(out=mag[:], in0=mag[:], scalar1=2.0 ** -116)
-
-        def emit_sign(eng, bank):
             nc.vector.scalar_tensor_tensor(
-                out=sgn[:], in0=noise_in[:], scalar=0.0, in1=neg[:], op0=ALU.is_gt, op1=ALU.subtract
+                out=sgn[:], in0=draws[:], scalar=0.0, in1=neg[:], op0=ALU.is_gt, op1=ALU.subtract
+            )
+            for cols in [slice(0, 8)] + [module_cols(j) for j in range(NM)]:
+                nc.gpsimd.tensor_tensor(out=root[:, cols], in0=mag[:, cols], in1=half[:, cols], op=ALU.pow)
+
+        def module_cols(j):
+            return slice(8 + CHUNKS * j, 8 + CHUNKS * (j + 1))
+
+        def factor(cols):
+            nc.vector.tensor_mul(out=fac[:, cols], in0=root[:, cols], in1=sgn[:, cols])
+
+        def spread_row_factor(h):
+            transpose_words(("fi", h), [fac[:, j : j + 1].to_broadcast([P, P]) for j in range(4 * h, 4 * h + 4)])
+
+        def keep_row_factor(h):
+            nc.scalar.copy(out=row_fac[:, 4 * h : 4 * h + 4, :], in_=bank_of[("fi", h)][:])
+
+        x1_g = keep.tile([P, NM * K], BF16, name="x1_g", align_bytes=64)
+        x1_c = keep.tile([P, NM * P], U32, name="x1_c", align_bytes=64)
+        x1_s = keep.tile([P, NM * P], U8, name="x1_s", align_bytes=64)
+
+        def x1_transpose(q):
+            src = x1_sb[q // 2]
+            transpose_words(("x1", q), halves(src[:, 2 * (q % 2), :]) + halves(src[:, 2 * (q % 2) + 1, :]))
+
+        def x1_regroup(q):
+            regroup("scalar", ("x1", q), x1_g[:, 2 * K * q : 2 * K * (q + 1)])
+
+        def x1_quantise(q):
+            nc.vector.quantize_mx(
+                out=x1_c[:, 2 * P * q : 2 * P * (q + 1)].bitcast(FP8X4),
+                scales=x1_s[:, 2 * P * q : 2 * P * (q + 1)],
+                in_=x1_g[:, 2 * K * q : 2 * K * (q + 1)],
             )
 
-        unit("TR", ("pe",), 130, -100, ["small"], emit_tr, bank="take", kind="t")
-        unit("EVR", ("dve",), 100, -100, ["TR"], emit_evr, bank="TR")
-        unit("chain", ("dve",), 700, -99, ["EVR"], emit_chain)
-        unit("sign", ("dve",), 70, -98, ["chain"], emit_sign, quick=True)
-        pieces = ((0, 8), (8, 12), (12, 16), (16, 24), (24, 40))
-        for i, (lo, hi) in enumerate(pieces):
+        w2_g = {}
+        w2_q = {}
 
-            def emit_pow(eng, bank, lo=lo, hi=hi):
-                nc.gpsimd.tensor_tensor(out=root[:, lo:hi], in0=mag[:, lo:hi], in1=half[:, lo:hi], op=ALU.pow)
+        def w2_transpose(m, j, hf):
+            src = w2_sb[m][j]
+            transpose_words(("w2", m, j, hf), halves(src[:, 2 * hf, :]) + halves(src[:, 2 * hf + 1, :]))
 
-            def emit_fac(eng, bank, lo=lo, hi=hi):
-                nc.vector.tensor_mul(out=fac[:, lo:hi], in0=root[:, lo:hi], in1=sgn[:, lo:hi])
+        def w2_regroup(engine, m, j, hf):
+            if hf == 0:
+                w2_g[(m, j)] = turn.tile([P, CHUNKS * K], BF16, name="w2_g%d" % m, align_bytes=64)
+            regroup(engine, ("w2", m, j, hf), w2_g[(m, j)][:, 2 * K * hf : 2 * K * (hf + 1)])
 
-            unit("pow%d" % i, ("pool",), 150 + 200 * (hi - lo), -97 + i, ["chain"], emit_pow)
-            unit("fac%d" % i, ("dve",), 70, (-97.0, -36.5, 63.5, 163.5, 363.5)[i], ["pow%d" % i, "sign"], emit_fac)
+        def w2_quantise(m, j):
+            w2_q[(m, j)] = quantise(w2_g[(m, j)][:], "w2_%d" % m, turn)
 
-        for h in range(2):
+        w3_g = {}
+        w3_q = {}
 
-            def emit_tfi(eng, bank, h=h):
-                ft = new_bank("TFI%d" % h, bank)
-                for jj in range(4):
-                    j = 4 * h + jj
-                    nc.tensor.transpose(ft[:, jj, :], fac[:, j : j + 1].to_broadcast([P, P]), ident[:])
+        def w3_transpose(j):
+            transpose_words(("w3", j), halves(w3_sb[0][j // 2][:, j % 2, :]) + halves(w3_sb[1][j // 2][:, j % 2, :]))
 
-            def emit_evfi(eng, bank, h=h):
-                copy_out(eng, fi_all[:, 4 * h : 4 * h + 4, :], banks["TFI%d" % h][:])
+        def w3_regroup(j):
+            w3_g[j] = turn.tile([P, 2 * K], BF16, name="w3_g", align_bytes=64)
+            regroup("scalar", ("w3", j), w3_g[j][:])
 
-            unit("TFI%d" % h, ("pe",), 300, -40 + 245 * h, ["fac0"], emit_tfi, bank="take", kind="t")
-            unit("EVFI%d" % h, ("act", "dve"), 445, -40 + 245 * h, ["TFI%d" % h], emit_evfi, bank="TFI%d" % h)
+        def w3_quantise(j):
+            w3_q[j] = quantise(w3_g[j][:], "w3_%d" % j, keep)
 
-        x1_g = work.tile([P, NM * K], BF16, name="x1_g", align_bytes=64)
-        x1_gw = x1_g[:].bitcast(F32).rearrange("p (j b u) -> p j b u", j=NM, u=2)
-        x1_c = work.tile([P, NM * P], U32, name="x1_c", align_bytes=64)
-        x1_s = work.tile([P, NM * P], U8, name="x1_s", align_bytes=64)
-        for q in range(4):
-
-            def emit_tx(eng, bank, q=q):
-                xt = new_bank("TX%d" % q, bank)
-                for jj in range(2):
-                    words = x1_sb[q][:, jj, :].bitcast(F32)
-                    for u in range(2):
-                        nc.tensor.transpose(xt[:, 2 * jj + u, :], words[:, P * u : P * u + P], ident[:])
-
-            def emit_evx(eng, bank, q=q):
-                copy_out(
-                    eng,
-                    x1_gw[:, 2 * q : 2 * q + 2],
-                    banks["TX%d" % q][:].rearrange("p (j u) b -> p j b u", u=2),
-                )
-
-            def emit_qx(eng, bank, q=q):
-                nc.vector.quantize_mx(
-                    out=x1_c[:, 256 * q : 256 * q + 256].bitcast(FP8X4),
-                    scales=x1_s[:, 256 * q : 256 * q + 256],
-                    in_=x1_g[:, 1024 * q : 1024 * q + 1024],
-                )
-
-            pr = 200 * q - 60
-            unit("TX%d" % q, ("pe",), 300, pr, ["x1_%d" % q], emit_tx, bank="take", kind="t")
-            unit("EVX%d" % q, ("act", "dve"), 445, pr, ["TX%d" % q], emit_evx, bank="TX%d" % q)
-            unit("QX%d" % q, ("dve",), 240, pr, ["EVX%d" % q], emit_qx)
-
-        g2 = {}
-        q2 = {}
-        g3 = {}
-        q3 = {}
         acc = {}
-        tmp = {}
-        x2q = {}
-        ps2 = {}
-        res = {}
-        for j in range(NM):
-            base = 100 * j
-            for m, off in ((1, 0), (0, 5)):
-                idx = 2 * j + (1 - m)
-                for hf in range(2):
+        hid = {}
+        x2_q = {}
 
-                    def emit_t2(eng, bank, j=j, m=m, hf=hf):
-                        xt = new_bank("T%d_%d_%d" % (m, j, hf), bank)
-                        for cc in range(2):
-                            words = w2_sb[m][j][:, 2 * hf + cc, :].bitcast(F32)
-                            for u in range(2):
-                                nc.tensor.transpose(xt[:, 2 * cc + u, :], words[:, P * u : P * u + P], ident[:])
-
-                    def emit_ev2(eng, bank, j=j, m=m, hf=hf, idx=idx):
-                        if (j, m) not in g2:
-                            g2[(j, m)] = work.tile(
-                                [P, 4 * K], BF16, name="w2_g", tag="w2_g%d" % (idx % N_G2), align_bytes=64
-                            )
-                        gw = g2[(j, m)][:].bitcast(F32).rearrange("p (c w u) -> p c w u", c=4, u=2)
-                        copy_out(
-                            eng,
-                            gw[:, 2 * hf : 2 * hf + 2],
-                            banks["T%d_%d_%d" % (m, j, hf)][:].rearrange("p (c u) w -> p c w u", u=2),
-                        )
-
-                    tn = "T%d_%d_%d" % (m, j, hf)
-                    deps = [tn]
-                    if idx >= N_G2:
-                        deps.append("Q%d_%d" % (1 - (idx - N_G2) % 2, (idx - N_G2) // 2))
-                    unit(tn, ("pe",), 300, base - 50 + off + hf, ["w2_%d_%d" % (m, j)], emit_t2, bank="take", kind="t")
-                    unit("EV%d_%d_%d" % (m, j, hf), ("act", "dve"), 445, base - 50 + off + hf, deps, emit_ev2, bank=tn)
-
-                def emit_q2(eng, bank, j=j, m=m, idx=idx):
-                    codes = work.tile([P, K], U32, name="w2_c", tag="w2_c%d" % (idx % N_C2), align_bytes=64)
-                    scales = work.tile([P, K], U8, name="w2_s", tag="w2_s%d" % (idx % N_C2), align_bytes=64)
-                    nc.vector.quantize_mx(out=codes[:].bitcast(FP8X4), scales=scales[:], in_=g2[(j, m)][:])
-                    q2[(j, m)] = (codes, scales)
-
-                deps = ["EV%d_%d_0" % (m, j), "EV%d_%d_1" % (m, j)]
-                if idx >= N_C2:
-                    deps.append("S1_%d_%d" % (1 - (idx - N_C2) % 2, (idx - N_C2) // 2))
-                unit("Q%d_%d" % (m, j), ("dve",), 477, base - 50 + off + 2, deps, emit_q2)
-
-                def emit_s1(eng, bank, j=j, m=m):
-                    codes, scales = q2[(j, m)]
-                    if m == 1:
-                        ps = psum.tile([P, 4, P], F32, name="ps_ls", tag="ls%d" % (j % N_LS))
-                    else:
-                        ps = psum.tile([P, 4, P], F32, name="ps_mu", tag="mu%d" % (j % N_MU))
-                    for c in range(4):
-                        nc.tensor.matmul_mx(
-                            out=ps[:, c, :],
-                            lhsT=codes[:, P * c : P * c + P].bitcast(FP8X4),
-                            lhsT_scale=scales[:, P * c : P * c + P],
-                            rhs=x1_c[:, P * j : P * j + P].bitcast(FP8X4),
-                            rhs_scale=x1_s[:, P * j : P * j + P],
-                            start=True,
-                            stop=True,
-                        )
-                    acc[(j, m)] = ps
-
-                deps = ["Q%d_%d" % (m, j), "QX%d" % (j // 2)]
-                if m == 1 and j >= N_LS:
-                    deps.append("a_%d" % (j - N_LS))
-                if m == 0 and j >= N_MU:
-                    deps.append("d_%d" % (j - N_MU))
-                unit("S1_%d_%d" % (m, j), ("pe",), 250, base - 40 + (1 - m), deps, emit_s1, kind="m")
-
-            def emit_t3(eng, bank, j=j):
-                xt = new_bank("TW3_%d" % j, bank)
-                for m in range(2):
-                    words = w3_sb[m][j // 2][:, j % 2, :].bitcast(F32)
-                    for u in range(2):
-                        nc.tensor.transpose(xt[:, 2 * m + u, :], words[:, P * u : P * u + P], ident[:])
-
-            def emit_ev3(eng, bank, j=j):
-                g3[j] = work.tile([P, 2 * K], BF16, name="w3_g", tag="w3_g%d" % (j % N_G3), align_bytes=64)
-                copy_out(
-                    eng,
-                    g3[j][:].bitcast(F32).rearrange("p (m o u) -> p m o u", m=2, u=2),
-                    banks["TW3_%d" % j][:].rearrange("p (m u) o -> p m o u", u=2),
+        def stage1(m, j):
+            tag = "ls" if m == LS else "mu%d" % (j % 2)
+            acc[(m, j)] = psum.tile([P, CHUNKS, P], F32, name="acc", tag=tag)
+            for c in range(CHUNKS):
+                pass_mx(
+                    acc[(m, j)][:, c, :], w2_q[(m, j)], (x1_c, x1_s), slice(P * c, P * (c + 1)), slice(P * j, P * (j + 1))
                 )
 
-            def emit_q3(eng, bank, j=j):
-                codes = work.tile([P, 2 * OUT], U32, name="w3_c%d" % j, align_bytes=64)
-                scales = work.tile([P, 2 * OUT], U8, name="w3_s%d" % j, align_bytes=64)
-                nc.vector.quantize_mx(out=codes[:].bitcast(FP8X4), scales=scales[:], in_=g3[j][:])
-                q3[j] = (codes, scales)
-
-            deps = ["TW3_%d" % j]
-            if j >= N_G3:
-                deps.append("QW3_%d" % (j - N_G3))
-            unit("TW3_%d" % j, ("pe",), 300, base - 20, ["w3_%d" % (j // 2)], emit_t3, bank="take", kind="t")
-            unit("EVW3_%d" % j, ("act", "dve"), 445, base - 20, deps, emit_ev3, bank="TW3_%d" % j)
-            unit("QW3_%d" % j, ("dve",), 240, base - 20, ["EVW3_%d" % j], emit_q3)
-
-            def emit_a(eng, bank, j=j):
-                e = work.tile([P, 4, P], F32, name="e", tag="e%d" % (j % 2))
-                for c in range(4):
-                    nc.scalar.activation(
-                        out=e[:, c, :],
-                        in_=acc[(j, 1)][:, c, :],
-                        func=ACT.Exp,
-                        bias=bias12[:, 1, j, c : c + 1],
-                        scale=1.0,
-                    )
-                tmp[("e", j)] = e
-
-            def emit_b(eng, bank, j=j):
-                t2 = work.tile([P, 4, P], F32, name="t2", tag="t2_%d" % (j % 2))
-                nc.vector.tensor_scalar(
-                    out=t2[:],
-                    in0=tmp[("e", j)][:],
-                    scalar1=clip_e[:, 0:1],
-                    scalar2=clip_e[:, 1:2],
-                    op0=ALU.max,
-                    op1=ALU.min,
-                )
-                tmp[("t2", j)] = t2
-
-            def emit_c(eng, bank, j=j):
-                t4 = work.tile([P, 4, P], F32, name="t4", tag="t4_%d" % (j % 2))
-                for c in range(4):
-                    nc.vector.scalar_tensor_tensor(
-                        out=t4[:, c, :],
-                        in0=tmp[("t2", j)][:, c, :],
-                        scalar=fac[:, 8 + 4 * j + c : 9 + 4 * j + c],
-                        in1=fi_all[:, j, :],
-                        op0=ALU.mult,
-                        op1=ALU.mult,
-                    )
-                tmp[("t4", j)] = t4
-
-            def emit_d(eng, bank, j=j):
-                s = work.tile([P, 4, P], F32, name="s", tag="s%d" % (j % 2))
-                for c in range(4):
-                    nc.vector.scalar_tensor_tensor(
-                        out=s[:, c, :],
-                        in0=acc[(j, 0)][:, c, :],
-                        scalar=bias12[:, 0, j, c : c + 1],
-                        in1=tmp[("t4", j)][:, c, :],
-                        op0=ALU.add,
-                        op1=ALU.add,
-                    )
-                tmp[("s", j)] = s
-
-            def emit_e(eng, bank, j=j):
-                x2_g = work.tile([P, K], BF16, name="x2_g", tag="x2_g%d" % (j % 2), align_bytes=64)
-                if eng == "act":
-                    nc.scalar.activation(
-                        out=x2_g[:].rearrange("p (b c) -> p b c", c=4),
-                        in_=tmp[("s", j)][:].rearrange("p c b -> p b c"),
-                        func=ACT.Relu,
-                    )
-                else:
-                    nc.vector.tensor_scalar_max(
-                        out=x2_g[:].rearrange("p (b c) -> p b c", c=4),
-                        in0=tmp[("s", j)][:].rearrange("p c b -> p b c"),
-                        scalar1=0.0,
-                    )
-                tmp[("x2", j)] = x2_g
-
-            def emit_qx2(eng, bank, j=j):
-                codes = work.tile([P, P], U32, name="x2_c%d" % j, align_bytes=64)
-                scales = work.tile([P, P], U8, name="x2_s%d" % j, align_bytes=64)
-                nc.vector.quantize_mx(out=codes[:].bitcast(FP8X4), scales=scales[:], in_=tmp[("x2", j)][:])
-                x2q[j] = (codes, scales)
-
-            def emit_s2(eng, bank, j=j):
-                if j % 2 == 0:
-                    ps2[j // 2] = psum.tile([P, 2, 2 * OUT], F32, name="ps2", tag="ps2")
-                codes, scales = x2q[j]
-                wc, ws = q3[j]
-                nc.tensor.matmul_mx(
-                    out=ps2[j // 2][:, j % 2, :],
-                    lhsT=codes[:].bitcast(FP8X4),
-                    lhsT_scale=scales[:],
-                    rhs=wc[:].bitcast(FP8X4),
-                    rhs_scale=ws[:],
-                    start=True,
-                    stop=True,
+        def sigma_exp(j):
+            hid[("e", j)] = turn.tile([P, CHUNKS, P], F32, name="e")
+            for c in range(CHUNKS):
+                nc.scalar.activation(
+                    out=hid[("e", j)][:, c, :],
+                    in_=acc[(LS, j)][:, c, :],
+                    func=ACT.Exp,
+                    bias=bias12[:, LS, j, c : c + 1],
+                    scale=1.0,
                 )
 
-            def emit_out(eng, bank, j=j):
-                q = j // 2
-                if j % 2 == 0:
-                    res[q] = work.tile([P, 2, 2, OUT], F32, name="res%d" % q)
-                r = res[q]
-                nc.vector.tensor_tensor(
-                    out=r[:, j % 2].rearrange("p m o -> p (m o)"),
-                    in0=ps2[q][:, j % 2, :],
-                    in1=bias3[:, j].rearrange("p m o -> p (m o)"),
-                    op=ALU.add,
-                )
-                if q == 3:
-                    nc.sync.dma_start(out=out_0[:, j, :], in_=r[:, j % 2, 0, :])
-                elif j % 2 == 1:
-                    nc.sync.dma_start(out=out_0[:, 2 * q : 2 * q + 2, :], in_=r[:, :, 0, :])
-
-            def emit_clip(eng, bank, j=j):
-                q = j // 2
-                r = res[q]
-                if q == 3:
-                    nc.vector.tensor_scalar(
-                        out=r[:, j % 2, 1, :], in0=r[:, j % 2, 1, :], scalar1=-20.0, scalar2=2.0, op0=ALU.max, op1=ALU.min
-                    )
-                    nc.sync.dma_start(out=out_1[:, j, :], in_=r[:, j % 2, 1, :])
-                else:
-                    nc.vector.tensor_scalar(
-                        out=r[:, :, 1, :], in0=r[:, :, 1, :], scalar1=-20.0, scalar2=2.0, op0=ALU.max, op1=ALU.min
-                    )
-                    nc.sync.dma_start(out=out_1[:, 2 * q : 2 * q + 2, :], in_=r[:, :, 1, :])
-
-            def older(name, back):
-                return [name % (j - back)] if j >= back else []
-
-            unit("a_%d" % j, ("act",), 600, base - 38, ["S1_1_%d" % j, "chain"] + older("b_%d", 2), emit_a)
-            unit("b_%d" % j, ("dve",), 226, base - 37, ["a_%d" % j] + older("c_%d", 2), emit_b)
-            unit(
-                "c_%d" % j,
-                ("dve",),
-                480,
-                base - 36,
-                ["b_%d" % j, "EVFI%d" % (j // 4), "fac%d" % (1 + min(j, 2) + (j // 4))] + older("d_%d", 2),
-                emit_c,
-                quick=True,
+        def sigma_clip(j):
+            hid[("sigma", j)] = turn.tile([P, CHUNKS, P], F32, name="sigma")
+            nc.vector.tensor_scalar(
+                out=hid[("sigma", j)][:],
+                in0=hid[("e", j)][:],
+                scalar1=clip_e[:, 0:1],
+                scalar2=clip_e[:, 1:2],
+                op0=ALU.max,
+                op1=ALU.min,
             )
-            unit("d_%d" % j, ("dve",), 480, base - 35, ["c_%d" % j, "S1_0_%d" % j] + older("e_%d", 2), emit_d)
-            unit("e_%d" % j, ("act",), 550, base - 34, ["d_%d" % j] + older("qx2_%d", 2), emit_e)
-            unit("qx2_%d" % j, ("dve",), 140, base - 33, ["e_%d" % j], emit_qx2)
-            deps = ["qx2_%d" % j, "QW3_%d" % j]
-            if j % 2 == 0 and j >= 2:
-                deps += ["OUT_%d" % (j - 1), "OUT_%d" % (j - 2)]
-            if j % 2 == 1:
-                deps.append("S2_%d" % (j - 1))
-            unit("S2_%d" % j, ("pe",), 111, base - 32, deps, emit_s2, kind="m")
-            unit("OUT_%d" % j, ("dve",), 230, base - 31, ["S2_%d" % j, "bias3"] + (older("OUT_%d", 1) if j % 2 == 1 else []), emit_out)
-            if j >= 6:
-                unit("CLIP_%d" % j, ("dve",), 70, base - 30, ["OUT_%d" % j], emit_clip)
-            elif j % 2 == 1:
-                unit("CLIP_%d" % j, ("dve",), 125, base - 30, ["OUT_%d" % j], emit_clip)
 
-        for name, eng, bank in plan(units, names, landed):
-            units[name]["emit"](eng, bank)
+        def noise_and_sum(j):
+            noisy = turn.tile([P, CHUNKS, P], F32, name="noisy")
+            hid[("sum", j)] = turn.tile([P, CHUNKS, P], F32, name="total")
+            for c in range(CHUNKS):
+                nc.vector.scalar_tensor_tensor(
+                    out=noisy[:, c, :],
+                    in0=hid[("sigma", j)][:, c, :],
+                    scalar=fac[:, 8 + CHUNKS * j + c : 9 + CHUNKS * j + c],
+                    in1=row_fac[:, j, :],
+                    op0=ALU.mult,
+                    op1=ALU.mult,
+                )
+            for c in range(CHUNKS):
+                nc.vector.scalar_tensor_tensor(
+                    out=hid[("sum", j)][:, c, :],
+                    in0=acc[(MU, j)][:, c, :],
+                    scalar=bias12[:, MU, j, c : c + 1],
+                    in1=noisy[:, c, :],
+                    op0=ALU.add,
+                    op1=ALU.add,
+                )
+
+        def relu_regroup(j):
+            hid[("x2", j)] = turn.tile([P, K], BF16, name="x2_g", align_bytes=64)
+            nc.scalar.activation(
+                out=hid[("x2", j)][:].rearrange("p (b c) -> p b c", c=CHUNKS),
+                in_=hid[("sum", j)][:].rearrange("p c b -> p b c"),
+                func=ACT.Relu,
+            )
+
+        def x2_quantise(j):
+            x2_q[j] = quantise(hid[("x2", j)][:], "x2_%d" % j, keep)
+
+        def stage2(q):
+            bank = next_bank(("heads", q))
+            for i in range(2):
+                j = 2 * q + i
+                pass_mx(
+                    bank[:, 2 * i : 2 * i + 2, :].rearrange("p m o -> p (m o)"),
+                    x2_q[j],
+                    w3_q[j],
+                    slice(0, P),
+                    slice(0, 2 * P),
+                )
+
+        def heads_out(q):
+            sums = bank_of[("heads", q)][:].rearrange("p (i m) o -> p i m o", m=2)
+            res = keep.tile([P, 2, 2, P], F32, name="res%d" % q)
+            pair = slice(2 * q, 2 * q + 2)
+            for m in (1, 0):
+                nc.vector.tensor_tensor(out=res[:, :, m, :], in0=sums[:, :, m, :], in1=bias3[:, pair, m, :], op=ALU.add)
+            nc.sync.dma_start(out=out_0[:, pair, :], in_=res[:, :, 0, :])
+            nc.vector.tensor_scalar(
+                out=res[:, :, 1, :], in0=res[:, :, 1, :], scalar1=-20.0, scalar2=2.0, op0=ALU.max, op1=ALU.min
+            )
+            nc.sync.dma_start(out=out_1[:, pair, :], in_=res[:, :, 1, :])
+
+        def live(j):
+            return 0 <= j < NM
+
+        small_vectors()
+        for q in range(NM // 2):
+            x1_transpose(q)
+            x1_regroup(q)
+        x1_quantise(0)
+        x1_quantise(1)
+
+        for j in range(-2, NM):
+            if live(j):
+                w3_transpose(j)
+            if live(j + 2):
+                w2_transpose(LS, j + 2, 0)
+                w2_transpose(LS, j + 2, 1)
+            if live(j):
+                sigma_clip(j)
+                factor(module_cols(j))
+            if live(j - 1):
+                x2_quantise(j - 1)
+            if live(j + 1):
+                w2_quantise(LS, j + 1)
+            if j == -1:
+                factor(slice(0, 8))
+            if live(j):
+                noise_and_sum(j)
+            if live(j + 1):
+                w2_regroup("scalar", MU, j + 1, 0)
+                w2_regroup("scalar", MU, j + 1, 1)
+            if live(j):
+                w3_regroup(j)
+            if live(j + 2):
+                w2_regroup("scalar", LS, j + 2, 0)
+            if live(j + 1):
+                stage1(LS, j + 1)
+            if j == -1:
+                spread_row_factor(0)
+                spread_row_factor(1)
+            if live(j + 2):
+                w2_transpose(MU, j + 2, 0)
+                w2_transpose(MU, j + 2, 1)
+            if live(j + 1):
+                w2_quantise(MU, j + 1)
+            if live(j + 2):
+                w2_regroup("vector", LS, j + 2, 1)
+            if j == -1:
+                x1_quantise(2)
+                x1_quantise(3)
+            if live(j + 1):
+                sigma_exp(j + 1)
+            if j == -1:
+                keep_row_factor(0)
+                keep_row_factor(1)
+            if live(j):
+                relu_regroup(j)
+                w3_quantise(j)
+            if live(j + 1):
+                stage1(MU, j + 1)
+
+        for q in range(NM // 2 - 1):
+            stage2(q)
+        heads_out(0)
+        x2_quantise(NM - 1)
+        stage2(NM // 2 - 1)
+        for q in range(1, NM // 2):
+            heads_out(q)

@@ -121,7 +121,23 @@ def tile_skill_net_pb_kernel(
         fac = keep.tile([P, 8 + CHUNKS * NM], F32, name="fac")
         row_fac = keep.tile([P, NM, P], F32, name="row_fac")
 
-        def small_vectors():
+        def noise_factors(cols, pieces):
+            x = draws[:, cols]
+            nc.vector.scalar_tensor_tensor(out=mag[:, cols], in0=x, scalar=-1.0, in1=x, op0=ALU.mult, op1=ALU.max)
+            nc.vector.tensor_single_scalar(out=neg[:, cols], in_=x, scalar=0.0, op=ALU.is_lt)
+            nc.vector.tensor_scalar_max(out=mag[:, cols], in0=mag[:, cols], scalar1=2.0 ** -116)
+            nc.vector.scalar_tensor_tensor(
+                out=sgn[:, cols], in0=x, scalar=0.0, in1=neg[:, cols], op0=ALU.is_gt, op1=ALU.subtract
+            )
+            for piece in pieces:
+                nc.gpsimd.tensor_tensor(out=root[:, piece], in0=mag[:, piece], in1=half[:, piece], op=ALU.pow)
+                nc.gpsimd.tensor_tensor(out=fac[:, piece], in0=root[:, piece], in1=sgn[:, piece], op=ALU.mult)
+
+        def row_draws():
+            nc.vector.tensor_copy(out=draws[:, 0:8], in_=ei_sb[:])
+            noise_factors(slice(0, 8), [slice(0, 8)])
+
+        def hidden_vectors():
             bank = next_bank("rows")
             for u, words in enumerate(halves(rows[:])):
                 nc.tensor.transpose(bank[:, u, :], words, ident[:])
@@ -129,25 +145,11 @@ def tile_skill_net_pb_kernel(
                 out=vec[:].bitcast(F32).rearrange("p (r u) -> p r u", u=2),
                 in_=bank[:, 0:2, 0:24].rearrange("p u r -> p r u"),
             )
-            nc.vector.tensor_copy(out=draws[:, 0:8], in_=ei_sb[:])
             nc.vector.tensor_copy(out=draws[:, 8:], in_=vec[:, 0 : CHUNKS * NM])
             nc.vector.tensor_copy(out=bias12[:].rearrange("p m j c -> p (m j c)"), in_=vec[:, CHUNKS * NM :])
-            nc.vector.scalar_tensor_tensor(
-                out=mag[:], in0=draws[:], scalar=-1.0, in1=draws[:], op0=ALU.mult, op1=ALU.max
+            noise_factors(
+                slice(8, 8 + CHUNKS * NM), [slice(8 + CHUNKS * j, 8 + CHUNKS * (j + 1)) for j in range(NM)]
             )
-            nc.vector.tensor_single_scalar(out=neg[:], in_=draws[:], scalar=0.0, op=ALU.is_lt)
-            nc.vector.tensor_scalar_max(out=mag[:], in0=mag[:], scalar1=2.0 ** -116)
-            nc.vector.scalar_tensor_tensor(
-                out=sgn[:], in0=draws[:], scalar=0.0, in1=neg[:], op0=ALU.is_gt, op1=ALU.subtract
-            )
-            for cols in [slice(0, 8)] + [module_cols(j) for j in range(NM)]:
-                nc.gpsimd.tensor_tensor(out=root[:, cols], in0=mag[:, cols], in1=half[:, cols], op=ALU.pow)
-
-        def module_cols(j):
-            return slice(8 + CHUNKS * j, 8 + CHUNKS * (j + 1))
-
-        def factor(cols):
-            nc.vector.tensor_mul(out=fac[:, cols], in0=root[:, cols], in1=sgn[:, cols])
 
         def spread_row_factor(h):
             transpose_words(("fi", h), [fac[:, j : j + 1].to_broadcast([P, P]) for j in range(4 * h, 4 * h + 4)])
@@ -295,14 +297,21 @@ def tile_skill_net_pb_kernel(
         def live(j):
             return 0 <= j < NM
 
-        small_vectors()
-        for q in range(NM // 2):
+        row_draws()
+        for q in (0, 1):
+            x1_transpose(q)
+            x1_regroup(q)
+        hidden_vectors()
+        for q in (2, 3):
             x1_transpose(q)
             x1_regroup(q)
         x1_quantise(0)
         x1_quantise(1)
 
         for j in range(-2, NM):
+            if live(j + 1):
+                w2_regroup("scalar", MU, j + 1, 0)
+                w2_regroup("scalar", MU, j + 1, 1)
             if live(j):
                 w3_transpose(j)
             if live(j + 2):
@@ -310,19 +319,12 @@ def tile_skill_net_pb_kernel(
                 w2_transpose(LS, j + 2, 1)
             if live(j):
                 sigma_clip(j)
-                factor(module_cols(j))
             if live(j - 1):
                 x2_quantise(j - 1)
             if live(j + 1):
                 w2_quantise(LS, j + 1)
-            if j == -1:
-                factor(slice(0, 8))
             if live(j):
                 noise_and_sum(j)
-            if live(j + 1):
-                w2_regroup("scalar", MU, j + 1, 0)
-                w2_regroup("scalar", MU, j + 1, 1)
-            if live(j):
                 w3_regroup(j)
             if live(j + 2):
                 w2_regroup("scalar", LS, j + 2, 0)

@@ -319,8 +319,6 @@ def tile_skill_net_pb_kernel(
                 w2_transpose(LS, j + 2, 1)
             if live(j):
                 sigma_clip(j)
-            if live(j - 1):
-                x2_quantise(j - 1)
             if live(j + 1):
                 w2_quantise(LS, j + 1)
             if live(j):
@@ -338,6 +336,8 @@ def tile_skill_net_pb_kernel(
                 w2_transpose(MU, j + 2, 1)
             if live(j + 1):
                 w2_quantise(MU, j + 1)
+            if live(j - 1):
+                x2_quantise(j - 1)
             if live(j + 2):
                 w2_regroup("vector", LS, j + 2, 1)
             if j == -1:

from contextlib import ExitStack

import concourse.mybir as mybir
from concourse.masks import make_identity

F32 = mybir.dt.float32
BF16 = mybir.dt.bfloat16
U32 = mybir.dt.uint32
U8 = mybir.dt.uint8
FP8X4 = mybir.dt.float8_e4m3fn_x4
ALU = mybir.AluOpType
ACT = mybir.ActivationFunctionType

P = 128
NM = 8
K = 512
CHUNKS = 4
MU, LS = 0, 1
N_BANKS = 5
FLOPS = 2 * P * NM * (2 * K * K + 2 * K * P)


def tile_skill_net_pb_kernel(
    tc, x1, ei2, ej2, w21, b21, w22, b22, w31, b31, w32, b32, out_0, out_1
):
    nc = tc.nc
    with ExitStack() as ctx:
        ctx.enter_context(tc.manual_schedule())
        keep = ctx.enter_context(tc.tile_pool(name="keep", bufs=1))
        turn = ctx.enter_context(tc.tile_pool(name="turn", bufs=2))
        psum = ctx.enter_context(tc.psum_pool(name="psum", bufs=1))

        rows = keep.tile([P, K], BF16, name="rows")
        ei_sb = keep.tile([P, NM], BF16, name="ei_sb")
        nc.scalar.dma_start(out=ei_sb[:], in_=ei2.rearrange("b j o -> b (j o)"))
        nc.scalar.dma_start(out=rows[0:8, :], in_=ej2.rearrange("o j h -> (o j) h"))
        nc.scalar.dma_start(out=rows[8:16, :], in_=b21)
        nc.scalar.dma_start(out=rows[16:24, :], in_=b22)
        nc.scalar.dma_start(out=rows[24:32, :], in_=b22)
        nc.vector.memset(rows[32:64, :], 0.0)
        nc.vector.memset(rows[64:128, :], 0.0)
        clip_in = keep.tile([P, 2], F32, name="clip_in")
        nc.vector.memset(clip_in[:, 0:1], -20.0)
        nc.vector.memset(clip_in[:, 1:2], 4.0)
        clip_e = keep.tile([P, 2], F32, name="clip_e")
        nc.scalar.activation(out=clip_e[:], in_=clip_in[:], func=ACT.Exp)
        half = keep.tile([P, 8 + CHUNKS * NM], F32, name="half")
        nc.vector.memset(half[:], 0.5)
        ident = keep.tile([P, P], F32, name="ident")
        make_identity(nc, ident[:])

        x1_sb = [keep.tile([P, 4, K], BF16, name="x1_sb%d" % h) for h in range(2)]
        w2_sb = [[keep.tile([P, CHUNKS, K], BF16, name="w2_sb%d_%d" % (m, j)) for j in range(NM)] for m in range(2)]
        w3_sb = [[keep.tile([P, 2, K], BF16, name="w3_sb%d_%d" % (m, q)) for q in range(NM // 2)] for m in range(2)]
        bias3 = keep.tile([P, NM, 2, P], BF16, name="bias3")
        for h in range(2):
            nc.sync.dma_start(out=x1_sb[h][:], in_=x1[:, 4 * h : 4 * h + 4, :])
        for j in range(NM):
            for m, w in ((LS, w22), (MU, w21)):
                nc.sync.dma_start(
                    out=w2_sb[m][j][:].rearrange("p (u e) k -> p u (e k)", u=2),
                    in_=w[j].rearrange("(u p e) k -> p u (e k)", u=2, e=2),
                )
            if j % 2 == 1:
                q = j // 2
                for m, w in ((0, w31), (1, w32)):
                    nc.sync.dma_start(out=w3_sb[m][q][:], in_=w[2 * q : 2 * q + 2].rearrange("j o h -> o j h"))
        nc.sync.dma_start(out=bias3[:, :, 0, :], in_=b31.partition_broadcast(P))
        nc.sync.dma_start(out=bias3[:, :, 1, :], in_=b32.partition_broadcast(P))

        banks_used = [0]
        bank_of = {}

        def next_bank(key):
            bank_of[key] = psum.tile([P, 4, P], F32, name="bank", tag="bank%d" % (banks_used[0] % N_BANKS))
            banks_used[0] += 1
            return bank_of[key]

        def transpose_words(key, sources):
            bank = next_bank(key)
            for i, words in enumerate(sources):
                nc.tensor.transpose(bank[:, i, :], words, ident[:])

        def halves(tile_2d):
            words = tile_2d.bitcast(F32)
            return [words[:, 0:P], words[:, P : 2 * P]]

        def regroup(engine, key, grouped):
            out = grouped.bitcast(F32).rearrange("p (i c u) -> p i c u", i=2, u=2)
            in_ = bank_of[key][:].rearrange("p (i u) c -> p i c u", u=2)
            if engine == "scalar":
                nc.scalar.copy(out=out, in_=in_)
            else:
                nc.vector.tensor_copy(out=out, in_=in_)

        def quantise(grouped, name, pool):
            width = grouped.shape[1] // 4
            codes = pool.tile([P, width], U32, name=name + "_c", align_bytes=64)
            scales = pool.tile([P, width], U8, name=name + "_s", align_bytes=64)
            nc.vector.quantize_mx(out=codes[:].bitcast(FP8X4), scales=scales[:], in_=grouped)
            return codes, scales

        def pass_mx(out, stationary, moving, s_cols, m_cols):
            nc.tensor.matmul_mx(
                out=out,
                lhsT=stationary[0][:, s_cols].bitcast(FP8X4),
                lhsT_scale=stationary[1][:, s_cols],
                rhs=moving[0][:, m_cols].bitcast(FP8X4),
                rhs_scale=moving[1][:, m_cols],
                start=True,
                stop=True,
            )

        vec = keep.tile([P, 24 * CHUNKS], BF16, name="vec")
        draws = keep.tile([P, 8 + CHUNKS * NM], F32, name="draws")
        bias12 = keep.tile([P, 2, NM, CHUNKS], F32, name="bias12")
        mag = keep.tile([P, 8 + CHUNKS * NM], F32, name="mag")
        neg = keep.tile([P, 8 + CHUNKS * NM], F32, name="neg")
        sgn = keep.tile([P, 8 + CHUNKS * NM], F32, name="sgn")
        root = keep.tile([P, 8 + CHUNKS * NM], F32, name="root")
        fac = keep.tile([P, 8 + CHUNKS * NM], F32, name="fac")
        row_fac = keep.tile([P, NM, P], F32, name="row_fac")

        def noise_factors(cols, pieces):
            x = draws[:, cols]
            nc.vector.scalar_tensor_tensor(out=mag[:, cols], in0=x, scalar=-1.0, in1=x, op0=ALU.mult, op1=ALU.max)
            nc.vector.tensor_single_scalar(out=neg[:, cols], in_=x, scalar=0.0, op=ALU.is_lt)
            nc.vector.tensor_scalar_max(out=mag[:, cols], in0=mag[:, cols], scalar1=2.0 ** -116)
            nc.vector.scalar_tensor_tensor(
                out=sgn[:, cols], in0=x, scalar=0.0, in1=neg[:, cols], op0=ALU.is_gt, op1=ALU.subtract
            )
            for piece in pieces:
                nc.gpsimd.tensor_tensor(out=root[:, piece], in0=mag[:, piece], in1=half[:, piece], op=ALU.pow)
                nc.gpsimd.tensor_tensor(out=fac[:, piece], in0=root[:, piece], in1=sgn[:, piece], op=ALU.mult)

        def row_draws():
            nc.vector.tensor_copy(out=draws[:, 0:8], in_=ei_sb[:])
            noise_factors(slice(0, 8), [slice(0, 8)])

        def hidden_vectors():
            bank = next_bank("rows")
            for u, words in enumerate(halves(rows[:])):
                nc.tensor.transpose(bank[:, u, :], words, ident[:])
            nc.vector.tensor_copy(
                out=vec[:].bitcast(F32).rearrange("p (r u) -> p r u", u=2),
                in_=bank[:, 0:2, 0:24].rearrange("p u r -> p r u"),
            )
            nc.vector.tensor_copy(out=draws[:, 8:], in_=vec[:, 0 : CHUNKS * NM])
            nc.vector.tensor_copy(out=bias12[:].rearrange("p m j c -> p (m j c)"), in_=vec[:, CHUNKS * NM :])
            noise_factors(
                slice(8, 8 + CHUNKS * NM), [slice(8 + CHUNKS * j, 8 + CHUNKS * (j + 1)) for j in range(NM)]
            )

        def spread_row_factor(h):
            transpose_words(("fi", h), [fac[:, j : j + 1].to_broadcast([P, P]) for j in range(4 * h, 4 * h + 4)])

        def keep_row_factor(h):
            nc.scalar.copy(out=row_fac[:, 4 * h : 4 * h + 4, :], in_=bank_of[("fi", h)][:])

        x1_g = keep.tile([P, NM * K], BF16, name="x1_g", align_bytes=64)
        x1_c = keep.tile([P, NM * P], U32, name="x1_c", align_bytes=64)
        x1_s = keep.tile([P, NM * P], U8, name="x1_s", align_bytes=64)

        def x1_transpose(q):
            src = x1_sb[q // 2]
            transpose_words(("x1", q), halves(src[:, 2 * (q % 2), :]) + halves(src[:, 2 * (q % 2) + 1, :]))

        def x1_regroup(q):
            regroup("scalar", ("x1", q), x1_g[:, 2 * K * q : 2 * K * (q + 1)])

        def x1_quantise(q):
            nc.vector.quantize_mx(
                out=x1_c[:, 2 * P * q : 2 * P * (q + 1)].bitcast(FP8X4),
                scales=x1_s[:, 2 * P * q : 2 * P * (q + 1)],
                in_=x1_g[:, 2 * K * q : 2 * K * (q + 1)],
            )

        w2_g = {}
        w2_q = {}

        def w2_transpose(m, j, hf):
            src = w2_sb[m][j]
            transpose_words(("w2", m, j, hf), halves(src[:, 2 * hf, :]) + halves(src[:, 2 * hf + 1, :]))

        def w2_regroup(engine, m, j, hf):
            if hf == 0:
                w2_g[(m, j)] = turn.tile([P, CHUNKS * K], BF16, name="w2_g%d" % m, align_bytes=64)
            regroup(engine, ("w2", m, j, hf), w2_g[(m, j)][:, 2 * K * hf : 2 * K * (hf + 1)])

        def w2_quantise(m, j):
            w2_q[(m, j)] = quantise(w2_g[(m, j)][:], "w2_%d" % m, turn)

        w3_g = {}
        w3_q = {}

        def w3_transpose(j):
            transpose_words(("w3", j), halves(w3_sb[0][j // 2][:, j % 2, :]) + halves(w3_sb[1][j // 2][:, j % 2, :]))

        def w3_regroup(j):
            w3_g[j] = turn.tile([P, 2 * K], BF16, name="w3_g", align_bytes=64)
            regroup("scalar", ("w3", j), w3_g[j][:])

        def w3_quantise(j):
            w3_q[j] = quantise(w3_g[j][:], "w3_%d" % j, keep)

        acc = {}
        hid = {}
        x2_q = {}

        def stage1(m, j):
            tag = "ls" if m == LS else "mu%d" % (j % 2)
            acc[(m, j)] = psum.tile([P, CHUNKS, P], F32, name="acc", tag=tag)
            for c in range(CHUNKS):
                pass_mx(
                    acc[(m, j)][:, c, :], w2_q[(m, j)], (x1_c, x1_s), slice(P * c, P * (c + 1)), slice(P * j, P * (j + 1))
                )

        def sigma_exp(j):
            hid[("e", j)] = turn.tile([P, CHUNKS, P], F32, name="e")
            for c in range(CHUNKS):
                nc.scalar.activation(
                    out=hid[("e", j)][:, c, :],
                    in_=acc[(LS, j)][:, c, :],
                    func=ACT.Exp,
                    bias=bias12[:, LS, j, c : c + 1],
                    scale=1.0,
                )

        def sigma_clip(j):
            hid[("sigma", j)] = turn.tile([P, CHUNKS, P], F32, name="sigma")
            nc.vector.tensor_scalar(
                out=hid[("sigma", j)][:],
                in0=hid[("e", j)][:],
                scalar1=clip_e[:, 0:1],
                scalar2=clip_e[:, 1:2],
                op0=ALU.max,
                op1=ALU.min,
            )

        def noise_and_sum(j):
            noisy = turn.tile([P, CHUNKS, P], F32, name="noisy")
            hid[("sum", j)] = turn.tile([P, CHUNKS, P], F32, name="total")
            for c in range(CHUNKS):
                nc.vector.scalar_tensor_tensor(
                    out=noisy[:, c, :],
                    in0=hid[("sigma", j)][:, c, :],
                    scalar=fac[:, 8 + CHUNKS * j + c : 9 + CHUNKS * j + c],
                    in1=row_fac[:, j, :],
                    op0=ALU.mult,
                    op1=ALU.mult,
                )
            for c in range(CHUNKS):
                nc.vector.scalar_tensor_tensor(
                    out=hid[("sum", j)][:, c, :],
                    in0=acc[(MU, j)][:, c, :],
                    scalar=bias12[:, MU, j, c : c + 1],
                    in1=noisy[:, c, :],
                    op0=ALU.add,
                    op1=ALU.add,
                )

        def relu_regroup(j):
            hid[("x2", j)] = turn.tile([P, K], BF16, name="x2_g", align_bytes=64)
            nc.scalar.activation(
                out=hid[("x2", j)][:].rearrange("p (b c) -> p b c", c=CHUNKS),
                in_=hid[("sum", j)][:].rearrange("p c b -> p b c"),
                func=ACT.Relu,
            )

        def x2_quantise(j):
            x2_q[j] = quantise(hid[("x2", j)][:], "x2_%d" % j, keep)

        def stage2(q):
            bank = next_bank(("heads", q))
            for i in range(2):
                j = 2 * q + i
                pass_mx(
                    bank[:, 2 * i : 2 * i + 2, :].rearrange("p m o -> p (m o)"),
                    x2_q[j],
                    w3_q[j],
                    slice(0, P),
                    slice(0, 2 * P),
                )

        def heads_out(q):
            sums = bank_of[("heads", q)][:].rearrange("p (i m) o -> p i m o", m=2)
            res = keep.tile([P, 2, 2, P], F32, name="res%d" % q)
            pair = slice(2 * q, 2 * q + 2)
            for m in (1, 0):
                nc.vector.tensor_tensor(out=res[:, :, m, :], in0=sums[:, :, m, :], in1=bias3[:, pair, m, :], op=ALU.add)
            nc.sync.dma_start(out=out_0[:, pair, :], in_=res[:, :, 0, :])
            nc.vector.tensor_scalar(
                out=res[:, :, 1, :], in0=res[:, :, 1, :], scalar1=-20.0, scalar2=2.0, op0=ALU.max, op1=ALU.min
            )
            nc.sync.dma_start(out=out_1[:, pair, :], in_=res[:, :, 1, :])

        def live(j):
            return 0 <= j < NM

        row_draws()
        for q in (0, 1):
            x1_transpose(q)
            x1_regroup(q)
        hidden_vectors()
        for q in (2, 3):
            x1_transpose(q)
            x1_regroup(q)
        x1_quantise(0)
        x1_quantise(1)

        for j in range(-2, NM):
            if live(j + 1):
                w2_regroup("scalar", MU, j + 1, 0)
                w2_regroup("scalar", MU, j + 1, 1)
            if live(j):
                w3_transpose(j)
            if live(j + 2):
                w2_transpose(LS, j + 2, 0)
                w2_transpose(LS, j + 2, 1)
            if live(j):
                sigma_clip(j)
            if live(j + 1):
                w2_quantise(LS, j + 1)
            if live(j):
                noise_and_sum(j)
                w3_regroup(j)
            if live(j + 2):
                w2_regroup("scalar", LS, j + 2, 0)
            if live(j + 1):
                stage1(LS, j + 1)
            if j == -1:
                spread_row_factor(0)
                spread_row_factor(1)
            if live(j + 2):
                w2_transpose(MU, j + 2, 0)
                w2_transpose(MU, j + 2, 1)
            if live(j + 1):
                w2_quantise(MU, j + 1)
            if live(j - 1):
                x2_quantise(j - 1)
            if live(j + 2):
                w2_regroup("vector", LS, j + 2, 1)
            if j == -1:
                x1_quantise(2)
                x1_quantise(3)
            if live(j + 1):
                sigma_exp(j + 1)
            if j == -1:
                keep_row_factor(0)
                keep_row_factor(1)
            if live(j):
                relu_regroup(j)
                w3_quantise(j)
            if live(j + 1):
                stage1(MU, j + 1)

        for q in range(NM // 2 - 1):
            stage2(q)
        heads_out(0)
        x2_quantise(NM - 1)
        stage2(NM // 2 - 1)
        for q in range(1, NM // 2):
            heads_out(q)
